import numpy as np
import ml_dtypes


def mxq(x, axis, fmt="e4m3"):
    dtype, down = {"e4m3": (ml_dtypes.float8_e4m3fn, 7), "e5m2": (ml_dtypes.float8_e5m2, 14)}[fmt]
    v = np.moveaxis(np.asarray(x, np.float32).astype(ml_dtypes.bfloat16).astype(np.float64), axis, -1)
    blocks = v.reshape(v.shape[:-1] + (-1, 32))
    amax = np.abs(blocks).max(-1, keepdims=True)
    byte = np.maximum(np.where(amax > 0, np.frexp(amax)[1] - 1 + 127, 0) - down, 1)
    scale = np.exp2(byte - 127.0)
    codes = (blocks / scale).astype(np.float32).astype(dtype).astype(np.float64)
    return np.moveaxis((codes * scale).reshape(v.shape), -1, axis)


WIDE = False


def mx_kscale(k):
    if not WIDE:
        return np.ones(k)
    levels = np.array([10, -10, 5, -5, 0])
    a = np.random.permutation(np.resize(levels, k // 512 * 4)).reshape(k // 512, 4)
    idx = np.arange(k)
    return np.exp2(a[idx // 512, idx % 128 // 32])


BF16 = ml_dtypes.bfloat16


def bf(x):
    return np.asarray(x, np.float32).astype(BF16)


def f64(x):
    return np.asarray(x).astype(np.float64)


B, DIM = 4096, 256
K = 2 * DIM


def sigmoid(v):
    return 1.0 / (1.0 + np.exp(-v))


def setup_inputs():
    s = mx_kscale(K)

    def w():
        return bf(np.random.standard_normal((DIM, K)) / np.sqrt(K) / s[None, :])

    def b():
        return bf(np.random.standard_normal(DIM) * 0.2)

    inp = {}
    inp["x"] = bf(np.random.standard_normal((B, DIM)) * s[:DIM])
    inp["h"] = bf(np.random.standard_normal((B, DIM)) * s[DIM:])
    inp["c"] = bf(np.random.standard_normal((B, DIM)))
    inp["n"] = bf(0.5 + np.random.uniform(0.0, 1.0, (B, DIM)))
    inp["m"] = bf(np.random.standard_normal((B, DIM)))
    for g in ("i", "f", "o", "z"):
        inp["W_" + g] = w()
        inp["b_" + g] = b()
    return inp


def reference(x, h, c, n, m, W_i, b_i, W_f, b_f, W_o, b_o, W_z, b_z):
    c, n, m = f64(c), f64(n), f64(m)
    combined = np.concatenate([f64(x), f64(h)], axis=-1)
    W = np.concatenate([f64(W_i), f64(W_f), f64(W_o), f64(W_z)], axis=0)
    b = np.concatenate([f64(b_i), f64(b_f), f64(b_o), f64(b_z)], axis=0)
    gates = (mxq(combined, 1, "e4m3") @ mxq(W, 1, "e4m3").T) + b
    i_t, f_t, o_t, z_t = np.split(gates, 4, axis=-1)
    z = np.tanh(z_t)
    m_new = np.maximum(f_t + m, i_t)
    i = np.exp(i_t - m_new)
    f = np.exp(f_t + m - m_new)
    c_new = f * c + i * z
    n_new = f * n + i
    h_new = sigmoid(o_t) * (c_new / (n_new + 1e-6))
    return np.stack([h_new, c_new, n_new, m_new])

@@ -1,0 +1,427 @@
+from contextlib import ExitStack
+
+import concourse.mybir as mybir
+from concourse.masks import make_identity
+
+F32 = mybir.dt.float32
+BF16 = mybir.dt.bfloat16
+U32 = mybir.dt.uint32
+U8 = mybir.dt.uint8
+FP8X4 = mybir.dt.float8_e4m3fn_x4
+ACT = mybir.ActivationFunctionType
+ALU = mybir.AluOpType
+
+P = 128
+B = 4096
+DIM = 256
+NT = B // P
+NQ = NT // 4
+NPAIR = NT // 2
+PW = 2 * DIM
+QW = 4 * DIM
+EPS = 1e-6
+FLOPS = 2 * B * 2 * DIM * 4 * DIM
+
+CHUNKS = [(0, 5), (5, 10), (10, 14), (14, 16)]
+P2_ON_GPSIMD = False
+NITER = 16 + 6
+GI, GF, GZ, GO = 0, 2, 4, 6
+LAG = 2
+BDELAY = 2
+
+
+def plan_b():
+    ln_at = {}
+    ready = {}
+    for ci, (s, e) in enumerate(CHUNKS):
+        ln_at[e + LAG - 1] = ci
+        for j in range(s, e):
+            ready[j] = e + LAG - 1 + BDELAY
+    b_at = {}
+    nxt = 0
+    for it in range(NITER):
+        b_at[it] = []
+        while nxt < NPAIR and ready[nxt] <= it:
+            b_at[it].append(nxt)
+            nxt += 1
+            if it < NPAIR + LAG - 1:
+                break
+    return ln_at, b_at
+
+
+def tile_slstmcell_t_kernel(tc, x, h, c, n, m, W_i, b_i, W_f, b_f, W_o, b_o, W_z, b_z, out):
+    nc = tc.nc
+    ln_at, b_at = plan_b()
+    b_it = {}
+    for it in b_at:
+        for j in b_at[it]:
+            b_it[j] = it
+    o_at = {}
+    for q in range(NQ):
+        o_at[q] = b_it[2 * q] - 2
+
+    xv = x.rearrange("(p t) d -> p (t d)", t=NT)
+    hv = h.rearrange("(p t) d -> p (t d)", t=NT)
+    cv = c.rearrange("(p t) d -> p (t d)", t=NT)
+    nv = n.rearrange("(p t) d -> p (t d)", t=NT)
+    mv = m.rearrange("(p t) d -> p (t d)", t=NT)
+    ov = out.rearrange("g (p t) d -> g p (t d)", t=NT)
+
+    with ExitStack() as ctx:
+        ctx.enter_context(tc.manual_schedule())
+        const = ctx.enter_context(tc.tile_pool(name="const", bufs=1))
+        ps = ctx.enter_context(tc.psum_pool(name="ps", bufs=1))
+        ld = ctx.enter_context(tc.tile_pool(name="ld", bufs=3))
+        grp = ctx.enter_context(tc.tile_pool(name="grp", bufs=3))
+
+        ident32 = const.tile([P, P], F32, name="ident32")
+        identb = const.tile([P, P], BF16, name="identb")
+        brow = const.tile([P, P], BF16, name="brow")
+        bcol = const.tile([P, 8], F32, name="bcol")
+        bhalf = const.tile([P, 2], F32, name="bhalf")
+        epsc = const.tile([P, 1], F32, name="epsc")
+        bfb = const.tile([P, DIM], BF16, name="bfb")
+        wc = const.tile([P, 8 * P], U32, name="wc", align_bytes=64)
+        wscl = const.tile([P, 8 * P], U8, name="wscl", align_bytes=64)
+        codes = const.tile([P, B], U32, name="codes", align_bytes=64)
+        scl = const.tile([P, B], U8, name="scl", align_bytes=64)
+
+        xq, hq, mq, cq, nq, mbq = {}, {}, {}, {}, {}, {}
+        gq = {}
+
+        def bank(tag):
+            return ps.tile([P, 512], F32, name="bank_" + tag, tag=tag, bufs=2 if tag == "T" else 1)
+
+        def load(dst, q, src, tag):
+            dst[q] = ld.tile([P, QW], BF16, name=tag + "q", tag=tag, bufs=4 if tag in ("x", "h") else 3)
+            nc.sync.dma_start(out=dst[q][:], in_=src[:, q * QW : (q + 1) * QW])
+
+        def e1(tag, ins, out32, eng):
+            tp = bank(tag)
+            for i, src in enumerate(ins):
+                nc.tensor.transpose(tp[:, i * P : (i + 1) * P], src, ident32[:])
+            src = tp[:].rearrange("p (s u c) -> p s c u", s=2, u=2)
+            if eng == "act":
+                nc.scalar.copy(out=out32, in_=src)
+            else:
+                nc.vector.tensor_copy(out=out32, in_=src)
+
+        def e1_pair(j, tag, eng):
+            q, jj = j // 2, j % 2
+            if jj == 0:
+                gq[q] = grp.tile([P, 4 * 512], BF16, name="g", tag="g", align_bytes=64)
+            x32 = xq[q][:].bitcast(F32)
+            h32 = hq[q][:].bitcast(F32)
+            ins = []
+            for tt in range(2):
+                t = 2 * jj + tt
+                ins.append(x32[:, t * P : (t + 1) * P])
+                ins.append(h32[:, t * P : (t + 1) * P])
+            g32 = gq[q][:].bitcast(F32).rearrange("p (t c u) -> p t c u", t=4, u=2)
+            e1(tag, ins, g32[:, 2 * jj : 2 * jj + 2], eng)
+
+        def quant(q):
+            nc.vector.quantize_mx(
+                out=codes[:, q * 512 : (q + 1) * 512].bitcast(FP8X4),
+                scales=scl[:, q * 512 : (q + 1) * 512],
+                in_=gq[q][:],
+            )
+
+        make_identity(nc, ident32[:])
+        nc.vector.memset(brow[:], 0.0)
+        nc.vector.memset(epsc[:], EPS)
+        nc.sync.dma_start(out=brow[0:2, :], in_=b_i.rearrange("(r c) -> r c", r=2))
+        nc.sync.dma_start(out=brow[4:6, :], in_=b_z.rearrange("(r c) -> r c", r=2))
+        nc.sync.dma_start(out=brow[6:8, :], in_=b_o.rearrange("(r c) -> r c", r=2))
+        nc.sync.dma_start(out=bfb[:], in_=b_f.partition_broadcast(P))
+        wst = ctx.enter_context(tc.tile_pool(name="wst", bufs=1))
+        w_sb = wst.tile([P, 8 * 512], BF16, name="w_sb")
+        gw = wst.tile([P, 8 * 512], BF16, name="gw", align_bytes=64)
+
+        def load_w(s0, wg):
+            nc.sync.dma_start(
+                out=w_sb[:, s0 * 512 : (s0 + 2) * 512].rearrange("p (r k) -> p r k", r=2),
+                in_=wg.rearrange("(r p) k -> p r k", p=P),
+            )
+
+        load_w(GI, W_i)
+        load_w(GF, W_f)
+        load(xq, 0, xv, "x")
+        load(hq, 0, hv, "h")
+        load(mq, 0, mv, "m")
+        load_w(GZ, W_z)
+        load(xq, 1, xv, "x")
+        load(hq, 1, hv, "h")
+        load(cq, 0, cv, "c")
+        load(nq, 0, nv, "n")
+        load_w(GO, W_o)
+        load(mq, 1, mv, "m")
+        load(xq, 2, xv, "x")
+        load(hq, 2, hv, "h")
+        load(cq, 1, cv, "c")
+        load(nq, 1, nv, "n")
+        load(xq, 3, xv, "x")
+        load(hq, 3, hv, "h")
+
+        nc.vector.tensor_copy(out=identb[:], in_=ident32[:])
+        tb = bank("E")
+        tbb = tb[:].bitcast(BF16)
+        nc.tensor.transpose(tbb[:, 0:P], brow[:], identb[:])
+        nc.vector.tensor_copy(out=bcol[:], in_=tbb[:, 0:8])
+        nc.vector.tensor_scalar(out=bhalf[:], in0=bcol[:, GO : GO + 2], scalar1=0.5, scalar2=None, op0=ALU.mult)
+        w32 = w_sb[:].bitcast(F32)
+        gw32 = gw[:].bitcast(F32).rearrange("p (s c u) -> p s c u", s=8, u=2)
+
+        def e1_w(k, tag, eng):
+            ins = [w32[:, (2 * k + s) * 256 + u * P : (2 * k + s) * 256 + (u + 1) * P] for s in range(2) for u in range(2)]
+            e1(tag, ins, gw32[:, 2 * k : 2 * k + 2], eng)
+
+        def quant_w(half):
+            nc.vector.quantize_mx(
+                out=wc[:, half * 512 : (half + 1) * 512].bitcast(FP8X4),
+                scales=wscl[:, half * 512 : (half + 1) * 512],
+                in_=gw[:, half * 2048 : (half + 1) * 2048],
+            )
+
+        e1_w(0, "T", "act")
+        e1_w(1, "T", "dve")
+        e1_pair(0, "Z", "act")
+        e1_pair(1, "TH", "dve")
+        quant_w(0)
+        quant(0)
+
+        gt = ctx.enter_context(tc.tile_pool(name="gt", bufs=2))
+        wk = ctx.enter_context(tc.tile_pool(name="wk", bufs=2))
+        ost = ctx.enter_context(tc.tile_pool(name="ost", bufs=3))
+        ring = ctx.enter_context(tc.tile_pool(name="ring", bufs=10))
+
+        iT, zT, thT = {}, {}, {}
+        Fb, TIb, Zb = {}, {}, {}
+        a_t, d_t, e1_t, e2_t = {}, {}, {}, {}
+        p_t, sq_t = {}, {}
+
+        def mxb(q, blk, dst, func, bias, scale, tag, bufs):
+            tbk = bank("T")
+            nc.tensor.matmul_mx(
+                out=tbk[:],
+                lhsT=wc[:, blk * P : (blk + 1) * P].bitcast(FP8X4),
+                lhsT_scale=wscl[:, blk * P : (blk + 1) * P],
+                rhs=codes[:, q * 512 : (q + 1) * 512].bitcast(FP8X4),
+                rhs_scale=scl[:, q * 512 : (q + 1) * 512],
+                start=True,
+                stop=True,
+            )
+            dst[(q, blk % 2)] = gt.tile([P, 512], F32, name=tag, tag=tag + str(blk % 2), bufs=bufs)
+            nc.scalar.activation(out=dst[(q, blk % 2)][:], in_=tbk[:], func=func, bias=bias, scale=scale)
+
+        def exit_i(q, r):
+            mxb(q, GI + r, iT, ACT.Identity, bcol[:, GI + r : GI + r + 1], 1.0, "iT", 2)
+
+        def exit_z(q, r):
+            mxb(q, GZ + r, zT, ACT.Tanh, bcol[:, GZ + r : GZ + r + 1], 1.0, "zT", 2)
+
+        def exit_o(q, r):
+            mxb(q, GO + r, thT, ACT.Tanh, bhalf[:, r : r + 1], 0.5, "thT", 3)
+
+        def back(tag, src, j):
+            q, jj = j // 2, j % 2
+            bk = bank(tag)
+            for tt in range(2):
+                for r in range(2):
+                    nc.tensor.transpose(
+                        bk[:, tt * DIM + r * P : tt * DIM + (r + 1) * P],
+                        src[(q, r)][:, (2 * jj + tt) * P : (2 * jj + tt + 1) * P],
+                        ident32[:],
+                    )
+            return bk
+
+        def pe_f(j):
+            Fb[j] = bank("F")
+            for tt in range(2):
+                t = 2 * j + tt
+                nc.tensor.matmul_mx(
+                    out=Fb[j][:, tt * DIM : (tt + 1) * DIM],
+                    lhsT=codes[:, t * P : (t + 1) * P].bitcast(FP8X4),
+                    lhsT_scale=scl[:, t * P : (t + 1) * P],
+                    rhs=wc[:, GF * P : (GF + 2) * P].bitcast(FP8X4),
+                    rhs_scale=wscl[:, GF * P : (GF + 2) * P],
+                    start=True,
+                    stop=True,
+                )
+
+        def mb(q, eng):
+            mbq[q] = wk.tile([P, QW], F32, name="mb", tag="mb")
+            eng.tensor_tensor(
+                out=mbq[q][:].rearrange("p (t d) -> p t d", t=4),
+                in0=mq[q][:].rearrange("p (t d) -> p t d", t=4),
+                in1=bfb[:].unsqueeze(1).to_broadcast([P, 4, DIM]),
+                op=ALU.add,
+            )
+
+        def pcols(j):
+            return slice((j % 2) * PW, (j % 2 + 1) * PW)
+
+        def store(g, j, t):
+            nc.sync.dma_start(out=ov[g, :, j * PW : (j + 1) * PW], in_=t[:])
+
+        def a1_a(j):
+            a_t[j] = wk.tile([P, PW], F32, name="a", tag="a")
+            nc.vector.tensor_tensor(out=a_t[j][:], in0=Fb[j][:], in1=mbq[j // 2][:, pcols(j)], op=ALU.add)
+
+        def a1_d(j):
+            d_t[j] = wk.tile([P, PW], F32, name="d", tag="d", bufs=3)
+            nc.vector.tensor_tensor(out=d_t[j][:], in0=TIb[j][:], in1=a_t[j][:], op=ALU.subtract)
+
+        def a1_mn(j):
+            mn = ost.tile([P, PW], F32, name="mn", tag="mn")
+            nc.vector.tensor_tensor(out=mn[:], in0=TIb[j][:], in1=a_t[j][:], op=ALU.max)
+            store(3, j, mn)
+
+        def exps(j):
+            e1_t[j] = wk.tile([P, PW], F32, name="e1", tag="e1", bufs=3)
+            e2_t[j] = wk.tile([P, PW], F32, name="e2", tag="e2", bufs=3)
+            nc.scalar.activation(out=e1_t[j][:], in_=d_t[j][:], func=ACT.Exp, scale=1.0)
+            nc.scalar.activation(out=e2_t[j][:], in_=d_t[j][:], func=ACT.Exp, scale=-1.0)
+
+        nn_t, iz_t, fn_t, fc_t, cn_t, p2_t = {}, {}, {}, {}, {}, {}
+
+        def a2_iz(j):
+            iz_t[j] = wk.tile([P, PW], F32, name="iz", tag="iz")
+            nc.vector.scalar_tensor_tensor(out=iz_t[j][:], in0=e1_t[j][:], scalar=1.0, in1=Zb[j][:], op0=ALU.min, op1=ALU.mult)
+
+        def a2_fn(j):
+            fn_t[j] = wk.tile([P, PW], F32, name="fn", tag="fn")
+            nc.vector.scalar_tensor_tensor(out=fn_t[j][:], in0=e2_t[j][:], scalar=1.0, in1=nq[j // 2][:, pcols(j)], op0=ALU.min, op1=ALU.mult)
+
+        def a2_fc(j):
+            fc_t[j] = wk.tile([P, PW], F32, name="fc", tag="fc")
+            nc.vector.scalar_tensor_tensor(out=fc_t[j][:], in0=e2_t[j][:], scalar=1.0, in1=cq[j // 2][:, pcols(j)], op0=ALU.min, op1=ALU.mult)
+
+        def a2_nn(j):
+            nn_t[j] = ost.tile([P, PW], F32, name="nn", tag="nn")
+            nc.vector.scalar_tensor_tensor(out=nn_t[j][:], in0=e1_t[j][:], scalar=1.0, in1=fn_t[j][:], op0=ALU.min, op1=ALU.add)
+            store(2, j, nn_t[j])
+
+        def a2_cn(j):
+            cn_t[j] = ost.tile([P, PW], F32, name="cn", tag="cn")
+            nc.vector.tensor_tensor(out=cn_t[j][:], in0=iz_t[j][:], in1=fc_t[j][:], op=ALU.add)
+            store(1, j, cn_t[j])
+
+        def a2_p(j):
+            p_t[j] = ring.tile([P, PW], F32, name="p", tag="p")
+            nc.vector.scalar_tensor_tensor(out=p_t[j][:], in0=nn_t[j][:], scalar=EPS, in1=cn_t[j][:], op0=ALU.add, op1=ALU.mult)
+
+        def sq(j):
+            sq_t[j] = ring.tile([P, PW], F32, name="sq", tag="sq")
+            nc.scalar.activation(out=sq_t[j][:], in_=nn_t[j][:], func=ACT.Square, bias=epsc[:], scale=1.0)
+
+        def ln(ci):
+            for j in range(CHUNKS[ci][0], CHUNKS[ci][1]):
+                nc.scalar.activation(out=sq_t[j][:], in_=sq_t[j][:], func=ACT.Ln, scale=2.0)
+
+        def r2(j):
+            nc.scalar.activation(out=sq_t[j][:], in_=sq_t[j][:], func=ACT.Exp, scale=-1.0)
+
+        def b_p2(j):
+            p2_t[j] = wk.tile([P, PW], F32, name="p2", tag="p2")
+            eng = nc.gpsimd if P2_ON_GPSIMD else nc.vector
+            eng.tensor_tensor(out=p2_t[j][:], in0=p_t[j][:], in1=sq_t[j][:], op=ALU.mult)
+
+        def b_h(j, thb):
+            hh = ost.tile([P, PW], F32, name="hh", tag="hh")
+            nc.vector.scalar_tensor_tensor(out=hh[:], in0=thb[:], scalar=1.0, in1=p2_t[j][:], op0=ALU.add, op1=ALU.mult)
+            store(0, j, hh)
+
+        mb(0, nc.vector)
+        exit_i(0, 0)
+        exit_i(0, 1)
+        pe_f(0)
+        TIb[0] = back("TI", iT, 0)
+
+        def startup(it):
+            if it == 0:
+                e1_pair(2, "TH", "dve")
+                e1_pair(3, "E", "dve")
+                e1_w(2, "Z", "act")
+                e1_w(3, "Z", "act")
+                e1_pair(4, "TH", "dve")
+                quant(1)
+                e1_pair(5, "E", "dve")
+                quant_w(1)
+                exit_z(0, 0)
+                exit_z(0, 1)
+            if it == 1:
+                quant(2)
+                e1_pair(6, "TH", "dve")
+                e1_pair(7, "E", "dve")
+
+        for it in range(NITER):
+            q, jj = it // 2, it % 2
+            j = it if it < NPAIR else None
+            k = it - LAG if 0 <= it - LAG < NPAIR else None
+            bs = b_at[it]
+            b = bs[0] if bs else None
+            thb = {}
+            if j is not None:
+                a1_a(j)
+            if k is not None:
+                a2_iz(k)
+            if j is not None:
+                a1_d(j)
+            startup(it)
+            if jj == 0 and q + 1 < NQ:
+                mb(q + 1, nc.gpsimd)
+                exit_i(q + 1, 0)
+                exit_i(q + 1, 1)
+            if jj == 1 and q + 1 < NQ:
+                exit_z(q + 1, 0)
+                exit_z(q + 1, 1)
+            if j is not None:
+                exps(j)
+            if k is not None:
+                a2_fn(k)
+            if j is not None:
+                a1_mn(j)
+            if it + 1 < NPAIR:
+                pe_f(it + 1)
+                TIb[it + 1] = back("TI", iT, it + 1)
+            zj = it - LAG + 1
+            if 0 <= zj < NPAIR:
+                Zb[zj] = back("Z", zT, zj)
+            if k is not None:
+                a2_fc(k)
+                a2_nn(k)
+                sq(k)
+                a2_cn(k)
+            if b is not None:
+                thb[b] = back("TH", thT, b)
+                b_p2(b)
+            if k is not None:
+                a2_p(k)
+            if b is not None:
+                b_h(b, thb[b])
+            for qo in range(NQ):
+                if o_at[qo] == it:
+                    exit_o(qo, 0)
+                    exit_o(qo, 1)
+            if 8 <= it + 5 < NPAIR:
+                e1_pair(it + 5, "E", "act")
+            for bb in b_at.get(it + 1, []):
+                r2(bb)
+            if it in ln_at:
+                ln(ln_at[it])
+            for bb in bs[1:]:
+                thb[bb] = back("TH", thT, bb)
+                b_p2(bb)
+                b_h(bb, thb[bb])
+            if jj == 1 and 3 <= q + 2 < NQ:
+                quant(q + 2)
+            if jj == 0:
+                if q + 4 < NQ:
+                    load(xq, q + 4, xv, "x")
+                    load(hq, q + 4, hv, "h")
+                if q + 2 < NQ:
+                    load(mq, q + 2, mv, "m")
+            if jj == 1 and q + 2 < NQ:
+                load(cq, q + 2, cv, "c")
+                load(nq, q + 2, nv, "n")

@@ -25,9 +25,9 @@ FLOPS = 2 * B * 2 * DIM * 4 * DIM
 CHUNKS = [(0, 5), (5, 10), (10, 14), (14, 16)]
 P2_ON_GPSIMD = False
 NITER = 16 + 6
-GI, GF, GZ, GO = 0, 2, 4, 6
+GI, GF, GZ, GO, GN = 0, 2, 4, 6, 8
 LAG = 2
-BDELAY = 2
+BDELAY = 3
 
 
 def plan_b():
@@ -58,7 +58,15 @@ def tile_slstmcell_t_kernel(tc, x, h, c, n, m, W_i, b_i, W_f, b_f, W_o, b_o, W_z
             b_it[j] = it
     o_at = {}
     for q in range(NQ):
-        o_at[q] = b_it[2 * q] - 2
+        o_at[q] = b_it[2 * q] - 3
+    ln_of = {}
+    for it in ln_at:
+        for j in range(CHUNKS[ln_at[it]][0], CHUNKS[ln_at[it]][1]):
+            ln_of[j] = it
+    r2_at = {}
+    for j in range(NPAIR):
+        at = max(b_it[j] - 2, ln_of[j] + 1)
+        r2_at[at] = r2_at.get(at, []) + [j]
 
     xv = x.rearrange("(p t) d -> p (t d)", t=NT)
     hv = h.rearrange("(p t) d -> p (t d)", t=NT)
@@ -79,10 +87,12 @@ def tile_slstmcell_t_kernel(tc, x, h, c, n, m, W_i, b_i, W_f, b_f, W_o, b_o, W_z
         brow = const.tile([P, P], BF16, name="brow")
         bcol = const.tile([P, 8], F32, name="bcol")
         bhalf = const.tile([P, 2], F32, name="bhalf")
+        bd = const.tile([P, 2], F32, name="bd")
+        negi = const.tile([P, P], BF16, name="negi")
         epsc = const.tile([P, 1], F32, name="epsc")
         bfb = const.tile([P, DIM], BF16, name="bfb")
-        wc = const.tile([P, 8 * P], U32, name="wc", align_bytes=64)
-        wscl = const.tile([P, 8 * P], U8, name="wscl", align_bytes=64)
+        wc = const.tile([P, 10 * P], U32, name="wc", align_bytes=64)
+        wscl = const.tile([P, 10 * P], U8, name="wscl", align_bytes=64)
         codes = const.tile([P, B], U32, name="codes", align_bytes=64)
         scl = const.tile([P, B], U8, name="scl", align_bytes=64)
 
@@ -90,7 +100,7 @@ def tile_slstmcell_t_kernel(tc, x, h, c, n, m, W_i, b_i, W_f, b_f, W_o, b_o, W_z
         gq = {}
 
         def bank(tag):
-            return ps.tile([P, 512], F32, name="bank_" + tag, tag=tag, bufs=2 if tag == "T" else 1)
+            return ps.tile([P, 512], F32, name="bank_" + tag, tag=tag, bufs=2 if tag == "T" else 6)
 
         def load(dst, q, src, tag):
             dst[q] = ld.tile([P, QW], BF16, name=tag + "q", tag=tag, bufs=4 if tag in ("x", "h") else 3)
@@ -131,12 +141,13 @@ def tile_slstmcell_t_kernel(tc, x, h, c, n, m, W_i, b_i, W_f, b_f, W_o, b_o, W_z
         nc.vector.memset(brow[:], 0.0)
         nc.vector.memset(epsc[:], EPS)
         nc.sync.dma_start(out=brow[0:2, :], in_=b_i.rearrange("(r c) -> r c", r=2))
+        nc.sync.dma_start(out=brow[2:4, :], in_=b_f.rearrange("(r c) -> r c", r=2))
         nc.sync.dma_start(out=brow[4:6, :], in_=b_z.rearrange("(r c) -> r c", r=2))
         nc.sync.dma_start(out=brow[6:8, :], in_=b_o.rearrange("(r c) -> r c", r=2))
         nc.sync.dma_start(out=bfb[:], in_=b_f.partition_broadcast(P))
         wst = ctx.enter_context(tc.tile_pool(name="wst", bufs=1))
         w_sb = wst.tile([P, 8 * 512], BF16, name="w_sb")
-        gw = wst.tile([P, 8 * 512], BF16, name="gw", align_bytes=64)
+        gw = wst.tile([P, 10 * 512], BF16, name="gw", align_bytes=64)
 
         def load_w(s0, wg):
             nc.sync.dma_start(
@@ -149,46 +160,50 @@ def tile_slstmcell_t_kernel(tc, x, h, c, n, m, W_i, b_i, W_f, b_f, W_o, b_o, W_z
         load(xq, 0, xv, "x")
         load(hq, 0, hv, "h")
         load(mq, 0, mv, "m")
-        load_w(GZ, W_z)
         load(xq, 1, xv, "x")
         load(hq, 1, hv, "h")
-        load(cq, 0, cv, "c")
-        load(nq, 0, nv, "n")
-        load_w(GO, W_o)
-        load(mq, 1, mv, "m")
+        load_w(GZ, W_z)
         load(xq, 2, xv, "x")
         load(hq, 2, hv, "h")
-        load(cq, 1, cv, "c")
-        load(nq, 1, nv, "n")
+        load(cq, 0, cv, "c")
+        load(nq, 0, nv, "n")
         load(xq, 3, xv, "x")
         load(hq, 3, hv, "h")
+        load(mq, 1, mv, "m")
+        load_w(GO, W_o)
+        load(cq, 1, cv, "c")
+        load(nq, 1, nv, "n")
 
         nc.vector.tensor_copy(out=identb[:], in_=ident32[:])
-        tb = bank("E")
+        nc.vector.tensor_scalar(out=negi[:], in0=ident32[:], scalar1=-1.0, scalar2=None, op0=ALU.mult)
+        tb = bank("B")
         tbb = tb[:].bitcast(BF16)
         nc.tensor.transpose(tbb[:, 0:P], brow[:], identb[:])
         nc.vector.tensor_copy(out=bcol[:], in_=tbb[:, 0:8])
         nc.vector.tensor_scalar(out=bhalf[:], in0=bcol[:, GO : GO + 2], scalar1=0.5, scalar2=None, op0=ALU.mult)
+        nc.vector.tensor_tensor(out=bd[:], in0=bcol[:, GI : GI + 2], in1=bcol[:, GF : GF + 2], op=ALU.subtract)
         w32 = w_sb[:].bitcast(F32)
-        gw32 = gw[:].bitcast(F32).rearrange("p (s c u) -> p s c u", s=8, u=2)
+        gw32 = gw[:, 0 : 8 * 512].bitcast(F32).rearrange("p (s c u) -> p s c u", s=8, u=2)
 
         def e1_w(k, tag, eng):
             ins = [w32[:, (2 * k + s) * 256 + u * P : (2 * k + s) * 256 + (u + 1) * P] for s in range(2) for u in range(2)]
             e1(tag, ins, gw32[:, 2 * k : 2 * k + 2], eng)
 
-        def quant_w(half):
+        def quant_w(s0, nblk):
             nc.vector.quantize_mx(
-                out=wc[:, half * 512 : (half + 1) * 512].bitcast(FP8X4),
-                scales=wscl[:, half * 512 : (half + 1) * 512],
-                in_=gw[:, half * 2048 : (half + 1) * 2048],
+                out=wc[:, s0 * P : (s0 + nblk) * P].bitcast(FP8X4),
+                scales=wscl[:, s0 * P : (s0 + nblk) * P],
+                in_=gw[:, s0 * 512 : (s0 + nblk) * 512],
             )
 
         e1_w(0, "T", "act")
         e1_w(1, "T", "dve")
-        e1_pair(0, "Z", "act")
-        e1_pair(1, "TH", "dve")
-        quant_w(0)
+        e1_pair(0, "B", "act")
+        e1_pair(1, "B", "dve")
+        nc.vector.tensor_scalar(out=gw[:, GN * 512 : (GN + 2) * 512], in0=gw[:, GF * 512 : (GF + 2) * 512], scalar1=-1.0, scalar2=None, op0=ALU.mult)
+        quant_w(GI, 4)
         quant(0)
+        quant_w(GN, 2)
 
         gt = ctx.enter_context(tc.tile_pool(name="gt", bufs=2))
         wk = ctx.enter_context(tc.tile_pool(name="wk", bufs=2))
@@ -200,22 +215,24 @@ def tile_slstmcell_t_kernel(tc, x, h, c, n, m, W_i, b_i, W_f, b_f, W_o, b_o, W_z
         a_t, d_t, e1_t, e2_t = {}, {}, {}, {}
         p_t, sq_t = {}, {}
 
-        def mxb(q, blk, dst, func, bias, scale, tag, bufs):
+        def mxb(q, blk, dst, func, bias, scale, tag, bufs, blk2=None):
             tbk = bank("T")
-            nc.tensor.matmul_mx(
-                out=tbk[:],
-                lhsT=wc[:, blk * P : (blk + 1) * P].bitcast(FP8X4),
-                lhsT_scale=wscl[:, blk * P : (blk + 1) * P],
-                rhs=codes[:, q * 512 : (q + 1) * 512].bitcast(FP8X4),
-                rhs_scale=scl[:, q * 512 : (q + 1) * 512],
-                start=True,
-                stop=True,
-            )
+            blks = [blk] if blk2 is None else [blk, blk2]
+            for n_, bl in enumerate(blks):
+                nc.tensor.matmul_mx(
+                    out=tbk[:],
+                    lhsT=wc[:, bl * P : (bl + 1) * P].bitcast(FP8X4),
+                    lhsT_scale=wscl[:, bl * P : (bl + 1) * P],
+                    rhs=codes[:, q * 512 : (q + 1) * 512].bitcast(FP8X4),
+                    rhs_scale=scl[:, q * 512 : (q + 1) * 512],
+                    start=(n_ == 0),
+                    stop=(n_ == len(blks) - 1),
+                )
             dst[(q, blk % 2)] = gt.tile([P, 512], F32, name=tag, tag=tag + str(blk % 2), bufs=bufs)
             nc.scalar.activation(out=dst[(q, blk % 2)][:], in_=tbk[:], func=func, bias=bias, scale=scale)
 
         def exit_i(q, r):
-            mxb(q, GI + r, iT, ACT.Identity, bcol[:, GI + r : GI + r + 1], 1.0, "iT", 2)
+            mxb(q, GI + r, iT, ACT.Identity, bd[:, r : r + 1], 1.0, "iT", 2, blk2=GN + r)
 
         def exit_z(q, r):
             mxb(q, GZ + r, zT, ACT.Tanh, bcol[:, GZ + r : GZ + r + 1], 1.0, "zT", 2)
@@ -235,8 +252,26 @@ def tile_slstmcell_t_kernel(tc, x, h, c, n, m, W_i, b_i, W_f, b_f, W_o, b_o, W_z
                     )
             return bk
 
+        def back_d(j):
+            q, jj = j // 2, j % 2
+            bk = bank("B")
+            for tt in range(2):
+                for r in range(2):
+                    cols = slice(tt * DIM + r * P, tt * DIM + (r + 1) * P)
+                    mcols = slice((2 * jj + tt) * DIM + r * P, (2 * jj + tt) * DIM + (r + 1) * P)
+                    nc.tensor.matmul(out=bk[:, cols], lhsT=negi[:], rhs=mq[q][:, mcols], start=True, stop=False)
+                    nc.tensor.matmul(
+                        out=bk[:, cols],
+                        lhsT=iT[(q, r)][:, (2 * jj + tt) * P : (2 * jj + tt + 1) * P],
+                        rhs=ident32[:],
+                        is_transpose=True,
+                        start=False,
+                        stop=True,
+                    )
+            return bk
+
         def pe_f(j):
-            Fb[j] = bank("F")
+            Fb[j] = bank("B")
             for tt in range(2):
                 t = 2 * j + tt
                 nc.tensor.matmul_mx(
@@ -268,20 +303,16 @@ def tile_slstmcell_t_kernel(tc, x, h, c, n, m, W_i, b_i, W_f, b_f, W_o, b_o, W_z
             a_t[j] = wk.tile([P, PW], F32, name="a", tag="a")
             nc.vector.tensor_tensor(out=a_t[j][:], in0=Fb[j][:], in1=mbq[j // 2][:, pcols(j)], op=ALU.add)
 
-        def a1_d(j):
-            d_t[j] = wk.tile([P, PW], F32, name="d", tag="d", bufs=3)
-            nc.vector.tensor_tensor(out=d_t[j][:], in0=TIb[j][:], in1=a_t[j][:], op=ALU.subtract)
-
         def a1_mn(j):
             mn = ost.tile([P, PW], F32, name="mn", tag="mn")
-            nc.vector.tensor_tensor(out=mn[:], in0=TIb[j][:], in1=a_t[j][:], op=ALU.max)
+            nc.vector.scalar_tensor_tensor(out=mn[:], in0=TIb[j][:], scalar=0.0, in1=a_t[j][:], op0=ALU.max, op1=ALU.add)
             store(3, j, mn)
 
         def exps(j):
             e1_t[j] = wk.tile([P, PW], F32, name="e1", tag="e1", bufs=3)
             e2_t[j] = wk.tile([P, PW], F32, name="e2", tag="e2", bufs=3)
-            nc.scalar.activation(out=e1_t[j][:], in_=d_t[j][:], func=ACT.Exp, scale=1.0)
-            nc.scalar.activation(out=e2_t[j][:], in_=d_t[j][:], func=ACT.Exp, scale=-1.0)
+            nc.scalar.activation(out=e1_t[j][:], in_=TIb[j][:], func=ACT.Exp, scale=1.0)
+            nc.scalar.activation(out=e2_t[j][:], in_=TIb[j][:], func=ACT.Exp, scale=-1.0)
 
         nn_t, iz_t, fn_t, fc_t, cn_t, p2_t = {}, {}, {}, {}, {}, {}
 
@@ -336,24 +367,43 @@ def tile_slstmcell_t_kernel(tc, x, h, c, n, m, W_i, b_i, W_f, b_f, W_o, b_o, W_z
         exit_i(0, 0)
         exit_i(0, 1)
         pe_f(0)
-        TIb[0] = back("TI", iT, 0)
+        TIb[0] = back_d(0)
 
         def startup(it):
             if it == 0:
-                e1_pair(2, "TH", "dve")
-                e1_pair(3, "E", "dve")
-                e1_w(2, "Z", "act")
-                e1_w(3, "Z", "act")
-                e1_pair(4, "TH", "dve")
+                e1_pair(2, "B", "dve")
+                e1_pair(3, "B", "dve")
+                e1_w(2, "B", "act")
+                e1_pair(4, "B", "dve")
                 quant(1)
-                e1_pair(5, "E", "dve")
-                quant_w(1)
+                quant_w(GZ, 2)
                 exit_z(0, 0)
                 exit_z(0, 1)
+                e1_pair(5, "B", "dve")
             if it == 1:
+                e1_pair(6, "B", "dve")
                 quant(2)
-                e1_pair(6, "TH", "dve")
-                e1_pair(7, "E", "dve")
+                e1_pair(7, "B", "dve")
+                e1_w(3, "B", "act")
+            if it == 2:
+                quant_w(GO, 2)
+
+        thb = {}
+
+        def fill_fz(it):
+            if it + 1 < NPAIR:
+                pe_f(it + 1)
+            zj = it - LAG + 1
+            if 0 <= zj < NPAIR:
+                Zb[zj] = back("B", zT, zj)
+
+        def fill_d(it):
+            if it + 1 < NPAIR:
+                TIb[it + 1] = back_d(it + 1)
+
+        def fill_th(it):
+            for bb in b_at.get(it + 1, [])[:1]:
+                thb[bb] = back("B", thT, bb)
 
         for it in range(NITER):
             q, jj = it // 2, it % 2
@@ -361,14 +411,41 @@ def tile_slstmcell_t_kernel(tc, x, h, c, n, m, W_i, b_i, W_f, b_f, W_o, b_o, W_z
             k = it - LAG if 0 <= it - LAG < NPAIR else None
             bs = b_at[it]
             b = bs[0] if bs else None
-            thb = {}
+            nxt = b_at.get(it + 1, [])
+            if it >= 2:
+                fill_fz(it)
             if j is not None:
                 a1_a(j)
+            if it >= 2:
+                fill_d(it)
             if k is not None:
                 a2_iz(k)
+            if it >= 2:
+                fill_th(it)
             if j is not None:
-                a1_d(j)
+                a1_mn(j)
+                exps(j)
             startup(it)
+            if it < 2:
+                fill_fz(it)
+                fill_d(it)
+            if k is not None:
+                a2_fn(k)
+                a2_fc(k)
+                a2_nn(k)
+                sq(k)
+            if b is not None:
+                b_p2(b)
+            if k is not None:
+                a2_cn(k)
+            if b is not None:
+                b_h(b, thb[b])
+            if k is not None:
+                a2_p(k)
+            for bb in bs[1:]:
+                thb[bb] = back("B", thT, bb)
+                b_p2(bb)
+                b_h(bb, thb[bb])
             if jj == 0 and q + 1 < NQ:
                 mb(q + 1, nc.gpsimd)
                 exit_i(q + 1, 0)
@@ -376,44 +453,16 @@ def tile_slstmcell_t_kernel(tc, x, h, c, n, m, W_i, b_i, W_f, b_f, W_o, b_o, W_z
             if jj == 1 and q + 1 < NQ:
                 exit_z(q + 1, 0)
                 exit_z(q + 1, 1)
-            if j is not None:
-                exps(j)
-            if k is not None:
-                a2_fn(k)
-            if j is not None:
-                a1_mn(j)
-            if it + 1 < NPAIR:
-                pe_f(it + 1)
-                TIb[it + 1] = back("TI", iT, it + 1)
-            zj = it - LAG + 1
-            if 0 <= zj < NPAIR:
-                Zb[zj] = back("Z", zT, zj)
-            if k is not None:
-                a2_fc(k)
-                a2_nn(k)
-                sq(k)
-                a2_cn(k)
-            if b is not None:
-                thb[b] = back("TH", thT, b)
-                b_p2(b)
-            if k is not None:
-                a2_p(k)
-            if b is not None:
-                b_h(b, thb[b])
             for qo in range(NQ):
                 if o_at[qo] == it:
                     exit_o(qo, 0)
                     exit_o(qo, 1)
             if 8 <= it + 5 < NPAIR:
-                e1_pair(it + 5, "E", "act")
-            for bb in b_at.get(it + 1, []):
+                e1_pair(it + 5, "T", "act")
+            for bb in r2_at.get(it, []):
                 r2(bb)
             if it in ln_at:
                 ln(ln_at[it])
-            for bb in bs[1:]:
-                thb[bb] = back("TH", thT, bb)
-                b_p2(bb)
-                b_h(bb, thb[bb])
             if jj == 1 and 3 <= q + 2 < NQ:
                 quant(q + 2)
             if jj == 0:

@@ -28,6 +28,7 @@ NITER = 16 + 6
 GI, GF, GZ, GO, GN = 0, 2, 4, 6, 8
 LAG = 2
 BDELAY = 3
+DUP = 1
 
 
 def plan_b():
@@ -218,6 +219,16 @@ def tile_slstmcell_t_kernel(tc, x, h, c, n, m, W_i, b_i, W_f, b_f, W_o, b_o, W_z
         def mxb(q, blk, dst, func, bias, scale, tag, bufs, blk2=None):
             tbk = bank("T")
             blks = [blk] if blk2 is None else [blk, blk2]
+            for n_ in range(DUP):
+                nc.tensor.matmul_mx(
+                    out=tbk[:],
+                    lhsT=wc[:, blk * P : (blk + 1) * P].bitcast(FP8X4),
+                    lhsT_scale=wscl[:, blk * P : (blk + 1) * P],
+                    rhs=codes[:, q * 512 : (q + 1) * 512].bitcast(FP8X4),
+                    rhs_scale=scl[:, q * 512 : (q + 1) * 512],
+                    start=True,
+                    stop=True,
+                )
             for n_, bl in enumerate(blks):
                 nc.tensor.matmul_mx(
                     out=tbk[:],
@@ -255,18 +266,16 @@ def tile_slstmcell_t_kernel(tc, x, h, c, n, m, W_i, b_i, W_f, b_f, W_o, b_o, W_z
         def back_d(j):
             q, jj = j // 2, j % 2
             bk = bank("B")
+            nc.tensor.matmul(out=bk[:], lhsT=negi[:], rhs=mq[q][:, jj * PW : (jj + 1) * PW], start=True, stop=False)
             for tt in range(2):
                 for r in range(2):
-                    cols = slice(tt * DIM + r * P, tt * DIM + (r + 1) * P)
-                    mcols = slice((2 * jj + tt) * DIM + r * P, (2 * jj + tt) * DIM + (r + 1) * P)
-                    nc.tensor.matmul(out=bk[:, cols], lhsT=negi[:], rhs=mq[q][:, mcols], start=True, stop=False)
                     nc.tensor.matmul(
-                        out=bk[:, cols],
+                        out=bk[:, tt * DIM + r * P : tt * DIM + (r + 1) * P],
                         lhsT=iT[(q, r)][:, (2 * jj + tt) * P : (2 * jj + tt + 1) * P],
                         rhs=ident32[:],
                         is_transpose=True,
                         start=False,
-                        stop=True,
+                        stop=(tt == 1 and r == 1),
                     )
             return bk
 

@@ -16,58 +16,27 @@ B = 4096
 DIM = 256
 NT = B // P
 NQ = NT // 4
-NPAIR = NT // 2
 PW = 2 * DIM
 QW = 4 * DIM
 EPS = 1e-6
 FLOPS = 2 * B * 2 * DIM * 4 * DIM
 
-CHUNKS = [(0, 5), (5, 10), (10, 14), (14, 16)]
+CHUNKS = [(0, 3), (3, 6), (6, 8)]
+B_AT = {5: [0], 6: [1], 7: [2], 8: [3, 4], 9: [5, 6, 7]}
+NITER = NQ + 2
+DUP = 0
 P2_ON_GPSIMD = False
-NITER = 16 + 6
+CN_ON_GPSIMD = False
+MB_ON_GPSIMD = True
 GI, GF, GZ, GO, GN = 0, 2, 4, 6, 8
-LAG = 2
-BDELAY = 3
-DUP = 1
-
-
-def plan_b():
-    ln_at = {}
-    ready = {}
-    for ci, (s, e) in enumerate(CHUNKS):
-        ln_at[e + LAG - 1] = ci
-        for j in range(s, e):
-            ready[j] = e + LAG - 1 + BDELAY
-    b_at = {}
-    nxt = 0
-    for it in range(NITER):
-        b_at[it] = []
-        while nxt < NPAIR and ready[nxt] <= it:
-            b_at[it].append(nxt)
-            nxt += 1
-            if it < NPAIR + LAG - 1:
-                break
-    return ln_at, b_at
+NRING = 6
 
 
 def tile_slstmcell_t_kernel(tc, x, h, c, n, m, W_i, b_i, W_f, b_f, W_o, b_o, W_z, b_z, out):
     nc = tc.nc
-    ln_at, b_at = plan_b()
-    b_it = {}
-    for it in b_at:
-        for j in b_at[it]:
-            b_it[j] = it
-    o_at = {}
-    for q in range(NQ):
-        o_at[q] = b_it[2 * q] - 3
-    ln_of = {}
-    for it in ln_at:
-        for j in range(CHUNKS[ln_at[it]][0], CHUNKS[ln_at[it]][1]):
-            ln_of[j] = it
-    r2_at = {}
-    for j in range(NPAIR):
-        at = max(b_it[j] - 2, ln_of[j] + 1)
-        r2_at[at] = r2_at.get(at, []) + [j]
+    ln_at = {}
+    for ci, (s, e) in enumerate(CHUNKS):
+        ln_at[e] = ci
 
     xv = x.rearrange("(p t) d -> p (t d)", t=NT)
     hv = h.rearrange("(p t) d -> p (t d)", t=NT)
@@ -81,55 +50,180 @@ def tile_slstmcell_t_kernel(tc, x, h, c, n, m, W_i, b_i, W_f, b_f, W_o, b_o, W_z
         const = ctx.enter_context(tc.tile_pool(name="const", bufs=1))
         ps = ctx.enter_context(tc.psum_pool(name="ps", bufs=1))
         ld = ctx.enter_context(tc.tile_pool(name="ld", bufs=3))
-        grp = ctx.enter_context(tc.tile_pool(name="grp", bufs=3))
+        grp = ctx.enter_context(tc.tile_pool(name="grp", bufs=2))
+        wst = ctx.enter_context(tc.tile_pool(name="wst", bufs=1))
+        gt = ctx.enter_context(tc.tile_pool(name="gt", bufs=2))
+        wk = ctx.enter_context(tc.tile_pool(name="wk", bufs=2))
+        ost = ctx.enter_context(tc.tile_pool(name="ost", bufs=2))
+        ring = ctx.enter_context(tc.tile_pool(name="ring", bufs=6))
 
         ident32 = const.tile([P, P], F32, name="ident32")
         identb = const.tile([P, P], BF16, name="identb")
+        negi = const.tile([P, P], BF16, name="negi")
         brow = const.tile([P, P], BF16, name="brow")
         bcol = const.tile([P, 8], F32, name="bcol")
         bhalf = const.tile([P, 2], F32, name="bhalf")
         bd = const.tile([P, 2], F32, name="bd")
-        negi = const.tile([P, P], BF16, name="negi")
         epsc = const.tile([P, 1], F32, name="epsc")
         bfb = const.tile([P, DIM], BF16, name="bfb")
+        bfrow = const.tile([P, DIM], BF16, name="bfrow")
+        ones = const.tile([P, P], BF16, name="ones")
         wc = const.tile([P, 10 * P], U32, name="wc", align_bytes=64)
         wscl = const.tile([P, 10 * P], U8, name="wscl", align_bytes=64)
         codes = const.tile([P, B], U32, name="codes", align_bytes=64)
         scl = const.tile([P, B], U8, name="scl", align_bytes=64)
+        w_sb = wst.tile([P, 8 * 512], BF16, name="w_sb")
+        gw = wst.tile([P, 10 * 512], BF16, name="gw", align_bytes=64)
 
-        xq, hq, mq, cq, nq, mbq = {}, {}, {}, {}, {}, {}
-        gq = {}
+        xq, hq, mq, cq, nq, mbq, gq = {}, {}, {}, {}, {}, {}, {}
+        dT, zT, thT = {}, {}, {}
+        e1q, e2q, fnq, nnq, cnq, mnq, hhq, pq, sqq, a_t = {}, {}, {}, {}, {}, {}, {}, {}, {}, {}
+        quantised = {}
 
-        def bank(tag):
-            return ps.tile([P, 512], F32, name="bank_" + tag, tag=tag, bufs=2 if tag == "T" else 6)
+        fills = []
+        state = {"filled": 0, "used": 0, "tpe": 0, "tact": 0}
+        bankof = {}
+        jobs = []
+
+        def pump():
+            while fills and state["filled"] - state["used"] < NRING:
+                if not fills[0]():
+                    break
+                fills.pop(0)
+                state["filled"] += 1
+
+        def used():
+            state["used"] += 1
+            pump()
+
+        def tpump():
+            while state["tpe"] < len(jobs) and state["tpe"] - state["tact"] < 2:
+                if not jobs[state["tpe"]][0]():
+                    break
+                state["tpe"] += 1
+
+        def tjob():
+            tpump()
+            assert state["tpe"] > state["tact"], "job not ready"
+            jobs[state["tact"]][1]()
+            state["tact"] += 1
+            tpump()
+            pump()
 
         def load(dst, q, src, tag):
-            dst[q] = ld.tile([P, QW], BF16, name=tag + "q", tag=tag, bufs=4 if tag in ("x", "h") else 3)
+            dst[q] = ld.tile([P, QW], BF16, name=tag + "q", tag=tag)
             nc.sync.dma_start(out=dst[q][:], in_=src[:, q * QW : (q + 1) * QW])
 
-        def e1(tag, ins, out32, eng):
-            tp = bank(tag)
-            for i, src in enumerate(ins):
-                nc.tensor.transpose(tp[:, i * P : (i + 1) * P], src, ident32[:])
-            src = tp[:].rearrange("p (s u c) -> p s c u", s=2, u=2)
-            if eng == "act":
-                nc.scalar.copy(out=out32, in_=src)
-            else:
-                nc.vector.tensor_copy(out=out32, in_=src)
+        def store(g, q, t):
+            nc.sync.dma_start(out=ov[g, :, q * QW : (q + 1) * QW], in_=t[:])
 
-        def e1_pair(j, tag, eng):
+        tb_of = {}
+
+        def add_e1(key, ins_fn, out_fn, eng, ready_fn):
+            def pe():
+                if not ready_fn():
+                    return False
+                tp = ps.tile([P, 512], F32, name="bank_T", tag="T", bufs=2)
+                tb_of[key] = tp
+                for i, src in enumerate(ins_fn()):
+                    nc.tensor.transpose(tp[:, i * P : (i + 1) * P], src, ident32[:])
+                return True
+
+            def drain():
+                src = tb_of[key][:].rearrange("p (s u c) -> p s c u", s=2, u=2)
+                if eng == "act":
+                    nc.scalar.copy(out=out_fn(), in_=src)
+                else:
+                    nc.vector.tensor_copy(out=out_fn(), in_=src)
+
+            jobs.append((pe, drain))
+
+        def add_e1_w(k, eng):
+            w32 = w_sb[:].bitcast(F32)
+            gw32 = gw[:, 0 : 8 * 512].bitcast(F32).rearrange("p (s c u) -> p s c u", s=8, u=2)
+            add_e1(
+                ("w", k),
+                lambda: [w32[:, (2 * k + s) * 256 + u * P : (2 * k + s) * 256 + (u + 1) * P] for s in range(2) for u in range(2)],
+                lambda: gw32[:, 2 * k : 2 * k + 2],
+                eng,
+                lambda: True,
+            )
+
+        def add_e1_pair(j, eng):
             q, jj = j // 2, j % 2
-            if jj == 0:
-                gq[q] = grp.tile([P, 4 * 512], BF16, name="g", tag="g", align_bytes=64)
-            x32 = xq[q][:].bitcast(F32)
-            h32 = hq[q][:].bitcast(F32)
-            ins = []
-            for tt in range(2):
-                t = 2 * jj + tt
-                ins.append(x32[:, t * P : (t + 1) * P])
-                ins.append(h32[:, t * P : (t + 1) * P])
-            g32 = gq[q][:].bitcast(F32).rearrange("p (t c u) -> p t c u", t=4, u=2)
-            e1(tag, ins, g32[:, 2 * jj : 2 * jj + 2], eng)
+
+            def ins():
+                x32 = xq[q][:].bitcast(F32)
+                h32 = hq[q][:].bitcast(F32)
+                res = []
+                for tt in range(2):
+                    t = 2 * jj + tt
+                    res.append(x32[:, t * P : (t + 1) * P])
+                    res.append(h32[:, t * P : (t + 1) * P])
+                return res
+
+            def dst():
+                if jj == 0:
+                    gq[q] = grp.tile([P, 4 * 512], BF16, name="g", tag="g", align_bytes=64)
+                g32 = gq[q][:].bitcast(F32).rearrange("p (t c u) -> p t c u", t=4, u=2)
+                return g32[:, 2 * jj : 2 * jj + 2]
+
+            add_e1(("x", j), ins, dst, eng, lambda: q in xq and q in hq)
+            if jj == 1 and q + 3 < NQ:
+                pe_, drain_ = jobs.pop()
+
+                def drain_and_load():
+                    drain_()
+                    load(xq, q + 3, xv, "x")
+                    load(hq, q + 3, hv, "h")
+
+                jobs.append((pe_, drain_and_load))
+
+        def add_exit(q, blk, dst, func, bias, scale, tag, bufs, blk2=None):
+            key = (tag, q, blk)
+
+            def pe():
+                if q not in quantised or blk not in quantised_w or (blk2 is not None and blk2 not in quantised_w):
+                    return False
+                tbk = ps.tile([P, 512], F32, name="bank_T", tag="T", bufs=2)
+                tb_of[key] = tbk
+                seq = [(blk, True, True)] * DUP
+                if blk2 is None:
+                    seq.append((blk, True, True))
+                else:
+                    seq.append((blk, True, False))
+                    seq.append((blk2, False, True))
+                for bl, st, sp in seq:
+                    nc.tensor.matmul_mx(
+                        out=tbk[:],
+                        lhsT=wc[:, bl * P : (bl + 1) * P].bitcast(FP8X4),
+                        lhsT_scale=wscl[:, bl * P : (bl + 1) * P],
+                        rhs=codes[:, q * 512 : (q + 1) * 512].bitcast(FP8X4),
+                        rhs_scale=scl[:, q * 512 : (q + 1) * 512],
+                        start=st,
+                        stop=sp,
+                    )
+                return True
+
+            def drain():
+                dst[(q, blk % 2)] = gt.tile([P, 512], F32, name=tag, tag=tag + str(blk % 2), bufs=bufs)
+                nc.scalar.activation(out=dst[(q, blk % 2)][:], in_=tb_of[key][:], func=func, bias=bias, scale=scale)
+
+            jobs.append((pe, drain))
+
+        quantised_w = {}
+
+        def add_exit_d(q):
+            for r in range(2):
+                add_exit(q, GI + r, dT, ACT.Identity, bd[:, r : r + 1], 1.0, "dT", 2, blk2=GN + r)
+
+        def add_exit_z(q):
+            for r in range(2):
+                add_exit(q, GZ + r, zT, ACT.Tanh, bcol[:, GZ + r : GZ + r + 1], 1.0, "zT", 2)
+
+        def add_exit_o(q):
+            for r in range(2):
+                add_exit(q, GO + r, thT, ACT.Tanh, bhalf[:, r : r + 1], 0.5, "thT", 3)
 
         def quant(q):
             nc.vector.quantize_mx(
@@ -137,18 +231,207 @@ def tile_slstmcell_t_kernel(tc, x, h, c, n, m, W_i, b_i, W_f, b_f, W_o, b_o, W_z
                 scales=scl[:, q * 512 : (q + 1) * 512],
                 in_=gq[q][:],
             )
+            quantised[q] = True
+            tpump()
+            pump()
+
+        def quant_w(s0, nblk):
+            nc.vector.quantize_mx(
+                out=wc[:, s0 * P : (s0 + nblk) * P].bitcast(FP8X4),
+                scales=wscl[:, s0 * P : (s0 + nblk) * P],
+                in_=gw[:, s0 * 512 : (s0 + nblk) * 512],
+            )
+            for bl in range(s0, s0 + nblk):
+                quantised_w[bl] = True
+            tpump()
+            pump()
+
+        def new_bank(key):
+            bankof[key] = ps.tile([P, 512], F32, name="bank_B", tag="B", bufs=NRING)
+            return bankof[key]
+
+        def add_f(j):
+            def go():
+                if j // 2 not in quantised or GF not in quantised_w:
+                    return False
+                bk = new_bank(("F", j))
+                for tt in range(2):
+                    t = 2 * j + tt
+                    nc.tensor.matmul_mx(
+                        out=bk[:, tt * DIM : (tt + 1) * DIM],
+                        lhsT=codes[:, t * P : (t + 1) * P].bitcast(FP8X4),
+                        lhsT_scale=scl[:, t * P : (t + 1) * P],
+                        rhs=wc[:, GF * P : (GF + 2) * P].bitcast(FP8X4),
+                        rhs_scale=wscl[:, GF * P : (GF + 2) * P],
+                        start=True,
+                        stop=True,
+                    )
+                return True
+
+            fills.append(go)
+
+        def add_back(kind, src, j, minus_m):
+            q, jj = j // 2, j % 2
+
+            def go():
+                if (q, 0) not in src or (q, 1) not in src:
+                    return False
+                bk = new_bank((kind, j))
+                if minus_m:
+                    nc.tensor.matmul(out=bk[:], lhsT=negi[:], rhs=mq[q][:, jj * PW : (jj + 1) * PW], start=True, stop=False)
+                for tt in range(2):
+                    for r in range(2):
+                        o = bk[:, tt * DIM + r * P : tt * DIM + (r + 1) * P]
+                        i = src[(q, r)][:, (2 * jj + tt) * P : (2 * jj + tt + 1) * P]
+                        if minus_m:
+                            nc.tensor.matmul(out=o, lhsT=i, rhs=ident32[:], is_transpose=True, start=False, stop=(tt == 1 and r == 1))
+                        else:
+                            nc.tensor.transpose(o, i, ident32[:])
+                return True
+
+            fills.append(go)
+
+        def half(t, j):
+            return t[:, (j % 2) * PW : (j % 2 + 1) * PW]
+
+        def mb(q, eng):
+            mbq[q] = wk.tile([P, QW], F32, name="mb", tag="mb")
+            for t in range(4):
+                cols = slice(t * DIM, (t + 1) * DIM)
+                eng.tensor_tensor(out=mbq[q][:, cols], in0=mq[q][:, cols], in1=bfb[:], op=ALU.add)
+
+        def v_a(j):
+            a_t[j] = wk.tile([P, PW], F32, name="a", tag="a")
+            nc.vector.tensor_tensor(out=a_t[j][:], in0=bankof[("F", j)][:], in1=half(mbq[j // 2], j), op=ALU.add)
+            used()
+
+        def v_mn(j):
+            q = j // 2
+            if j % 2 == 0:
+                mnq[q] = ost.tile([P, QW], F32, name="mn", tag="mn")
+                e1q[q] = wk.tile([P, QW], F32, name="e1", tag="e1")
+                e2q[q] = wk.tile([P, QW], F32, name="e2", tag="e2")
+            d = bankof[("D", j)]
+            nc.vector.scalar_tensor_tensor(out=half(mnq[q], j), in0=d[:], scalar=0.0, in1=a_t[j][:], op0=ALU.max, op1=ALU.add)
+            nc.scalar.activation(out=half(e1q[q], j), in_=d[:], func=ACT.Exp, scale=1.0)
+            nc.scalar.activation(out=half(e2q[q], j), in_=d[:], func=ACT.Exp, scale=-1.0)
+            used()
+            if j % 2 == 1:
+                store(3, q, mnq[q])
+
+        def v_fn(q):
+            fnq[q] = wk.tile([P, QW], F32, name="fn", tag="fn")
+            nc.vector.scalar_tensor_tensor(out=fnq[q][:], in0=e2q[q][:], scalar=1.0, in1=nq[q][:], op0=ALU.min, op1=ALU.mult)
+
+        def v_nn(q):
+            nnq[q] = ost.tile([P, QW], F32, name="nn", tag="nn", bufs=3 if CN_ON_GPSIMD else 2)
+            nc.vector.scalar_tensor_tensor(out=nnq[q][:], in0=e1q[q][:], scalar=1.0, in1=fnq[q][:], op0=ALU.min, op1=ALU.add)
+            store(2, q, nnq[q])
+            sqq[q] = ring.tile([P, QW], F32, name="sq", tag="sq")
+            nc.scalar.activation(out=sqq[q][:], in_=nnq[q][:], func=ACT.Square, bias=epsc[:], scale=1.0)
+
+        def v_fc(q):
+            nc.vector.scalar_tensor_tensor(out=e2q[q][:], in0=e2q[q][:], scalar=1.0, in1=cq[q][:], op0=ALU.min, op1=ALU.mult)
+
+        def v_iz(j):
+            e1h = half(e1q[j // 2], j)
+            nc.vector.scalar_tensor_tensor(out=e1h, in0=e1h, scalar=1.0, in1=bankof[("Z", j)][:], op0=ALU.min, op1=ALU.mult)
+            used()
+
+        def v_cn(q):
+            cnq[q] = ost.tile([P, QW], F32, name="cn", tag="cn", bufs=3 if CN_ON_GPSIMD else 2)
+            if CN_ON_GPSIMD:
+                for t in range(4):
+                    cols = slice(t * DIM, (t + 1) * DIM)
+                    nc.gpsimd.tensor_tensor(out=cnq[q][:, cols], in0=e1q[q][:, cols], in1=e2q[q][:, cols], op=ALU.add)
+            else:
+                nc.vector.tensor_tensor(out=cnq[q][:], in0=e1q[q][:], in1=e2q[q][:], op=ALU.add)
+            store(1, q, cnq[q])
+
+        r2done, p2done = {}, {}
+
+        def g_p2(q):
+            if P2_ON_GPSIMD and q in pq and q in r2done and q not in p2done:
+                p2done[q] = True
+                for t in range(4):
+                    cols = slice(t * DIM, (t + 1) * DIM)
+                    nc.gpsimd.tensor_tensor(out=sqq[q][:, cols], in0=pq[q][:, cols], in1=sqq[q][:, cols], op=ALU.mult)
+
+        def v_p(q):
+            pq[q] = ring.tile([P, QW], F32, name="p", tag="p")
+            nc.vector.scalar_tensor_tensor(out=pq[q][:], in0=nnq[q][:], scalar=EPS, in1=cnq[q][:], op0=ALU.add, op1=ALU.mult)
+            g_p2(q)
+
+        def s_ln(ci):
+            for q in range(CHUNKS[ci][0], CHUNKS[ci][1]):
+                nc.scalar.activation(out=sqq[q][:], in_=sqq[q][:], func=ACT.Ln, scale=2.0)
+
+        def s_r2(q):
+            nc.scalar.activation(out=sqq[q][:], in_=sqq[q][:], func=ACT.Exp, scale=-1.0)
+            r2done[q] = True
+            g_p2(q)
+
+        def v_p2(q):
+            if not P2_ON_GPSIMD:
+                nc.vector.tensor_tensor(out=sqq[q][:], in0=pq[q][:], in1=sqq[q][:], op=ALU.mult)
+
+        def v_h(j):
+            q = j // 2
+            if j % 2 == 0:
+                hhq[q] = ost.tile([P, QW], F32, name="hh", tag="hh")
+            nc.vector.scalar_tensor_tensor(out=half(hhq[q], j), in0=bankof[("TH", j)][:], scalar=1.0, in1=half(sqq[q], j), op0=ALU.add, op1=ALU.mult)
+            used()
+            if j % 2 == 1:
+                store(0, q, hhq[q])
+
+        add_e1_w(0, "act")
+        add_e1_w(1, "dve")
+        add_e1_pair(0, "act")
+        add_e1_pair(1, "dve")
+        add_exit_d(0)
+        add_e1_pair(2, "dve")
+        add_e1_pair(3, "dve")
+        add_e1_w(2, "act")
+        add_e1_pair(4, "dve")
+        add_e1_pair(5, "dve")
+        per_it = {}
+        for it in range(NITER):
+            n0 = len(jobs)
+            if it + 1 < NQ:
+                add_exit_d(it + 1)
+            if it < NQ:
+                add_exit_z(it)
+            for bq in B_AT.get(it + 1, []):
+                add_exit_o(bq)
+            if it + 3 < NQ:
+                add_e1_pair(2 * (it + 3), "act")
+                add_e1_pair(2 * (it + 3) + 1, "act")
+            if it == 0:
+                add_e1_w(3, "act")
+            per_it[it] = len(jobs) - n0
+        for it in range(NITER):
+            if it < NQ:
+                add_f(2 * it)
+                add_f(2 * it + 1)
+                add_back("D", dT, 2 * it, True)
+                add_back("D", dT, 2 * it + 1, True)
+            if 1 <= it <= NQ:
+                add_back("Z", zT, 2 * (it - 1), False)
+                add_back("Z", zT, 2 * (it - 1) + 1, False)
+            for bq in B_AT.get(it, []):
+                add_back("TH", thT, 2 * bq, False)
+                add_back("TH", thT, 2 * bq + 1, False)
 
         make_identity(nc, ident32[:])
         nc.vector.memset(brow[:], 0.0)
         nc.vector.memset(epsc[:], EPS)
-        nc.sync.dma_start(out=brow[0:2, :], in_=b_i.rearrange("(r c) -> r c", r=2))
-        nc.sync.dma_start(out=brow[2:4, :], in_=b_f.rearrange("(r c) -> r c", r=2))
-        nc.sync.dma_start(out=brow[4:6, :], in_=b_z.rearrange("(r c) -> r c", r=2))
-        nc.sync.dma_start(out=brow[6:8, :], in_=b_o.rearrange("(r c) -> r c", r=2))
-        nc.sync.dma_start(out=bfb[:], in_=b_f.partition_broadcast(P))
-        wst = ctx.enter_context(tc.tile_pool(name="wst", bufs=1))
-        w_sb = wst.tile([P, 8 * 512], BF16, name="w_sb")
-        gw = wst.tile([P, 10 * 512], BF16, name="gw", align_bytes=64)
+        nc.vector.memset(bfrow[:], 0.0)
+        nc.vector.memset(ones[:], 1.0)
+        nc.scalar.dma_start(out=brow[0:2, :], in_=b_i.rearrange("(r c) -> r c", r=2))
+        nc.scalar.dma_start(out=brow[2:4, :], in_=b_f.rearrange("(r c) -> r c", r=2))
+        nc.scalar.dma_start(out=bfrow[0:1, :], in_=b_f.rearrange("(r c) -> r c", r=1))
+        nc.scalar.dma_start(out=brow[4:6, :], in_=b_z.rearrange("(r c) -> r c", r=2))
+        nc.scalar.dma_start(out=brow[6:8, :], in_=b_o.rearrange("(r c) -> r c", r=2))
 
         def load_w(s0, wg):
             nc.sync.dma_start(
@@ -168,318 +451,116 @@ def tile_slstmcell_t_kernel(tc, x, h, c, n, m, W_i, b_i, W_f, b_f, W_o, b_o, W_z
         load(hq, 2, hv, "h")
         load(cq, 0, cv, "c")
         load(nq, 0, nv, "n")
-        load(xq, 3, xv, "x")
-        load(hq, 3, hv, "h")
         load(mq, 1, mv, "m")
         load_w(GO, W_o)
-        load(cq, 1, cv, "c")
-        load(nq, 1, nv, "n")
 
         nc.vector.tensor_copy(out=identb[:], in_=ident32[:])
         nc.vector.tensor_scalar(out=negi[:], in0=ident32[:], scalar1=-1.0, scalar2=None, op0=ALU.mult)
-        tb = bank("B")
+        tjob()
+        tjob()
+        nc.vector.tensor_scalar(out=gw[:, GN * 512 : (GN + 2) * 512], in0=gw[:, GF * 512 : (GF + 2) * 512], scalar1=-1.0, scalar2=None, op0=ALU.mult)
+        quant_w(GI, 4)
+        tjob()
+        tjob()
+        tb = ps.tile([P, 512], F32, name="bank_B", tag="B", bufs=NRING)
         tbb = tb[:].bitcast(BF16)
         nc.tensor.transpose(tbb[:, 0:P], brow[:], identb[:])
         nc.vector.tensor_copy(out=bcol[:], in_=tbb[:, 0:8])
+        nc.tensor.matmul(out=tb[:, DIM : 2 * DIM], lhsT=ones[:], rhs=bfrow[:], start=True, stop=True)
+        nc.vector.tensor_copy(out=bfb[:], in_=tb[:, DIM : 2 * DIM])
         nc.vector.tensor_scalar(out=bhalf[:], in0=bcol[:, GO : GO + 2], scalar1=0.5, scalar2=None, op0=ALU.mult)
         nc.vector.tensor_tensor(out=bd[:], in0=bcol[:, GI : GI + 2], in1=bcol[:, GF : GF + 2], op=ALU.subtract)
-        w32 = w_sb[:].bitcast(F32)
-        gw32 = gw[:, 0 : 8 * 512].bitcast(F32).rearrange("p (s c u) -> p s c u", s=8, u=2)
+        state["filled"] += 1
+        state["used"] += 1
 
-        def e1_w(k, tag, eng):
-            ins = [w32[:, (2 * k + s) * 256 + u * P : (2 * k + s) * 256 + (u + 1) * P] for s in range(2) for u in range(2)]
-            e1(tag, ins, gw32[:, 2 * k : 2 * k + 2], eng)
-
-        def quant_w(s0, nblk):
-            nc.vector.quantize_mx(
-                out=wc[:, s0 * P : (s0 + nblk) * P].bitcast(FP8X4),
-                scales=wscl[:, s0 * P : (s0 + nblk) * P],
-                in_=gw[:, s0 * 512 : (s0 + nblk) * 512],
-            )
-
-        e1_w(0, "T", "act")
-        e1_w(1, "T", "dve")
-        e1_pair(0, "B", "act")
-        e1_pair(1, "B", "dve")
-        nc.vector.tensor_scalar(out=gw[:, GN * 512 : (GN + 2) * 512], in0=gw[:, GF * 512 : (GF + 2) * 512], scalar1=-1.0, scalar2=None, op0=ALU.mult)
-        quant_w(GI, 4)
-        quant(0)
         quant_w(GN, 2)
-
-        gt = ctx.enter_context(tc.tile_pool(name="gt", bufs=2))
-        wk = ctx.enter_context(tc.tile_pool(name="wk", bufs=2))
-        ost = ctx.enter_context(tc.tile_pool(name="ost", bufs=3))
-        ring = ctx.enter_context(tc.tile_pool(name="ring", bufs=10))
-
-        iT, zT, thT = {}, {}, {}
-        Fb, TIb, Zb = {}, {}, {}
-        a_t, d_t, e1_t, e2_t = {}, {}, {}, {}
-        p_t, sq_t = {}, {}
-
-        def mxb(q, blk, dst, func, bias, scale, tag, bufs, blk2=None):
-            tbk = bank("T")
-            blks = [blk] if blk2 is None else [blk, blk2]
-            for n_ in range(DUP):
-                nc.tensor.matmul_mx(
-                    out=tbk[:],
-                    lhsT=wc[:, blk * P : (blk + 1) * P].bitcast(FP8X4),
-                    lhsT_scale=wscl[:, blk * P : (blk + 1) * P],
-                    rhs=codes[:, q * 512 : (q + 1) * 512].bitcast(FP8X4),
-                    rhs_scale=scl[:, q * 512 : (q + 1) * 512],
-                    start=True,
-                    stop=True,
-                )
-            for n_, bl in enumerate(blks):
-                nc.tensor.matmul_mx(
-                    out=tbk[:],
-                    lhsT=wc[:, bl * P : (bl + 1) * P].bitcast(FP8X4),
-                    lhsT_scale=wscl[:, bl * P : (bl + 1) * P],
-                    rhs=codes[:, q * 512 : (q + 1) * 512].bitcast(FP8X4),
-                    rhs_scale=scl[:, q * 512 : (q + 1) * 512],
-                    start=(n_ == 0),
-                    stop=(n_ == len(blks) - 1),
-                )
-            dst[(q, blk % 2)] = gt.tile([P, 512], F32, name=tag, tag=tag + str(blk % 2), bufs=bufs)
-            nc.scalar.activation(out=dst[(q, blk % 2)][:], in_=tbk[:], func=func, bias=bias, scale=scale)
-
-        def exit_i(q, r):
-            mxb(q, GI + r, iT, ACT.Identity, bd[:, r : r + 1], 1.0, "iT", 2, blk2=GN + r)
-
-        def exit_z(q, r):
-            mxb(q, GZ + r, zT, ACT.Tanh, bcol[:, GZ + r : GZ + r + 1], 1.0, "zT", 2)
-
-        def exit_o(q, r):
-            mxb(q, GO + r, thT, ACT.Tanh, bhalf[:, r : r + 1], 0.5, "thT", 3)
-
-        def back(tag, src, j):
-            q, jj = j // 2, j % 2
-            bk = bank(tag)
-            for tt in range(2):
-                for r in range(2):
-                    nc.tensor.transpose(
-                        bk[:, tt * DIM + r * P : tt * DIM + (r + 1) * P],
-                        src[(q, r)][:, (2 * jj + tt) * P : (2 * jj + tt + 1) * P],
-                        ident32[:],
-                    )
-            return bk
-
-        def back_d(j):
-            q, jj = j // 2, j % 2
-            bk = bank("B")
-            nc.tensor.matmul(out=bk[:], lhsT=negi[:], rhs=mq[q][:, jj * PW : (jj + 1) * PW], start=True, stop=False)
-            for tt in range(2):
-                for r in range(2):
-                    nc.tensor.matmul(
-                        out=bk[:, tt * DIM + r * P : tt * DIM + (r + 1) * P],
-                        lhsT=iT[(q, r)][:, (2 * jj + tt) * P : (2 * jj + tt + 1) * P],
-                        rhs=ident32[:],
-                        is_transpose=True,
-                        start=False,
-                        stop=(tt == 1 and r == 1),
-                    )
-            return bk
-
-        def pe_f(j):
-            Fb[j] = bank("B")
-            for tt in range(2):
-                t = 2 * j + tt
-                nc.tensor.matmul_mx(
-                    out=Fb[j][:, tt * DIM : (tt + 1) * DIM],
-                    lhsT=codes[:, t * P : (t + 1) * P].bitcast(FP8X4),
-                    lhsT_scale=scl[:, t * P : (t + 1) * P],
-                    rhs=wc[:, GF * P : (GF + 2) * P].bitcast(FP8X4),
-                    rhs_scale=wscl[:, GF * P : (GF + 2) * P],
-                    start=True,
-                    stop=True,
-                )
-
-        def mb(q, eng):
-            mbq[q] = wk.tile([P, QW], F32, name="mb", tag="mb")
-            eng.tensor_tensor(
-                out=mbq[q][:].rearrange("p (t d) -> p t d", t=4),
-                in0=mq[q][:].rearrange("p (t d) -> p t d", t=4),
-                in1=bfb[:].unsqueeze(1).to_broadcast([P, 4, DIM]),
-                op=ALU.add,
-            )
-
-        def pcols(j):
-            return slice((j % 2) * PW, (j % 2 + 1) * PW)
-
-        def store(g, j, t):
-            nc.sync.dma_start(out=ov[g, :, j * PW : (j + 1) * PW], in_=t[:])
-
-        def a1_a(j):
-            a_t[j] = wk.tile([P, PW], F32, name="a", tag="a")
-            nc.vector.tensor_tensor(out=a_t[j][:], in0=Fb[j][:], in1=mbq[j // 2][:, pcols(j)], op=ALU.add)
-
-        def a1_mn(j):
-            mn = ost.tile([P, PW], F32, name="mn", tag="mn")
-            nc.vector.scalar_tensor_tensor(out=mn[:], in0=TIb[j][:], scalar=0.0, in1=a_t[j][:], op0=ALU.max, op1=ALU.add)
-            store(3, j, mn)
-
-        def exps(j):
-            e1_t[j] = wk.tile([P, PW], F32, name="e1", tag="e1", bufs=3)
-            e2_t[j] = wk.tile([P, PW], F32, name="e2", tag="e2", bufs=3)
-            nc.scalar.activation(out=e1_t[j][:], in_=TIb[j][:], func=ACT.Exp, scale=1.0)
-            nc.scalar.activation(out=e2_t[j][:], in_=TIb[j][:], func=ACT.Exp, scale=-1.0)
-
-        nn_t, iz_t, fn_t, fc_t, cn_t, p2_t = {}, {}, {}, {}, {}, {}
-
-        def a2_iz(j):
-            iz_t[j] = wk.tile([P, PW], F32, name="iz", tag="iz")
-            nc.vector.scalar_tensor_tensor(out=iz_t[j][:], in0=e1_t[j][:], scalar=1.0, in1=Zb[j][:], op0=ALU.min, op1=ALU.mult)
-
-        def a2_fn(j):
-            fn_t[j] = wk.tile([P, PW], F32, name="fn", tag="fn")
-            nc.vector.scalar_tensor_tensor(out=fn_t[j][:], in0=e2_t[j][:], scalar=1.0, in1=nq[j // 2][:, pcols(j)], op0=ALU.min, op1=ALU.mult)
-
-        def a2_fc(j):
-            fc_t[j] = wk.tile([P, PW], F32, name="fc", tag="fc")
-            nc.vector.scalar_tensor_tensor(out=fc_t[j][:], in0=e2_t[j][:], scalar=1.0, in1=cq[j // 2][:, pcols(j)], op0=ALU.min, op1=ALU.mult)
-
-        def a2_nn(j):
-            nn_t[j] = ost.tile([P, PW], F32, name="nn", tag="nn")
-            nc.vector.scalar_tensor_tensor(out=nn_t[j][:], in0=e1_t[j][:], scalar=1.0, in1=fn_t[j][:], op0=ALU.min, op1=ALU.add)
-            store(2, j, nn_t[j])
-
-        def a2_cn(j):
-            cn_t[j] = ost.tile([P, PW], F32, name="cn", tag="cn")
-            nc.vector.tensor_tensor(out=cn_t[j][:], in0=iz_t[j][:], in1=fc_t[j][:], op=ALU.add)
-            store(1, j, cn_t[j])
-
-        def a2_p(j):
-            p_t[j] = ring.tile([P, PW], F32, name="p", tag="p")
-            nc.vector.scalar_tensor_tensor(out=p_t[j][:], in0=nn_t[j][:], scalar=EPS, in1=cn_t[j][:], op0=ALU.add, op1=ALU.mult)
-
-        def sq(j):
-            sq_t[j] = ring.tile([P, PW], F32, name="sq", tag="sq")
-            nc.scalar.activation(out=sq_t[j][:], in_=nn_t[j][:], func=ACT.Square, bias=epsc[:], scale=1.0)
-
-        def ln(ci):
-            for j in range(CHUNKS[ci][0], CHUNKS[ci][1]):
-                nc.scalar.activation(out=sq_t[j][:], in_=sq_t[j][:], func=ACT.Ln, scale=2.0)
-
-        def r2(j):
-            nc.scalar.activation(out=sq_t[j][:], in_=sq_t[j][:], func=ACT.Exp, scale=-1.0)
-
-        def b_p2(j):
-            p2_t[j] = wk.tile([P, PW], F32, name="p2", tag="p2")
-            eng = nc.gpsimd if P2_ON_GPSIMD else nc.vector
-            eng.tensor_tensor(out=p2_t[j][:], in0=p_t[j][:], in1=sq_t[j][:], op=ALU.mult)
-
-        def b_h(j, thb):
-            hh = ost.tile([P, PW], F32, name="hh", tag="hh")
-            nc.vector.scalar_tensor_tensor(out=hh[:], in0=thb[:], scalar=1.0, in1=p2_t[j][:], op0=ALU.add, op1=ALU.mult)
-            store(0, j, hh)
-
+        quant(0)
         mb(0, nc.vector)
-        exit_i(0, 0)
-        exit_i(0, 1)
-        pe_f(0)
-        TIb[0] = back_d(0)
+        tjob()
+        tjob()
+        pump()
 
-        def startup(it):
-            if it == 0:
-                e1_pair(2, "B", "dve")
-                e1_pair(3, "B", "dve")
-                e1_w(2, "B", "act")
-                e1_pair(4, "B", "dve")
+        def startup(it, pos):
+            if it == 0 and pos == 0:
+                tjob()
+                tjob()
+                tjob()
+                tjob()
+                tjob()
+            if it == 0 and pos == 1:
                 quant(1)
                 quant_w(GZ, 2)
-                exit_z(0, 0)
-                exit_z(0, 1)
-                e1_pair(5, "B", "dve")
-            if it == 1:
-                e1_pair(6, "B", "dve")
                 quant(2)
-                e1_pair(7, "B", "dve")
-                e1_w(3, "B", "act")
-            if it == 2:
+            if it == 1 and pos == 3:
                 quant_w(GO, 2)
 
-        thb = {}
-
-        def fill_fz(it):
-            if it + 1 < NPAIR:
-                pe_f(it + 1)
-            zj = it - LAG + 1
-            if 0 <= zj < NPAIR:
-                Zb[zj] = back("B", zT, zj)
-
-        def fill_d(it):
-            if it + 1 < NPAIR:
-                TIb[it + 1] = back_d(it + 1)
-
-        def fill_th(it):
-            for bb in b_at.get(it + 1, [])[:1]:
-                thb[bb] = back("B", thT, bb)
-
         for it in range(NITER):
-            q, jj = it // 2, it % 2
-            j = it if it < NPAIR else None
-            k = it - LAG if 0 <= it - LAG < NPAIR else None
-            bs = b_at[it]
-            b = bs[0] if bs else None
-            nxt = b_at.get(it + 1, [])
-            if it >= 2:
-                fill_fz(it)
-            if j is not None:
-                a1_a(j)
-            if it >= 2:
-                fill_d(it)
-            if k is not None:
-                a2_iz(k)
-            if it >= 2:
-                fill_th(it)
-            if j is not None:
-                a1_mn(j)
-                exps(j)
-            startup(it)
-            if it < 2:
-                fill_fz(it)
-                fill_d(it)
-            if k is not None:
-                a2_fn(k)
-                a2_fc(k)
-                a2_nn(k)
-                sq(k)
-            if b is not None:
-                b_p2(b)
-            if k is not None:
-                a2_cn(k)
-            if b is not None:
-                b_h(b, thb[b])
-            if k is not None:
-                a2_p(k)
-            for bb in bs[1:]:
-                thb[bb] = back("B", thT, bb)
-                b_p2(bb)
-                b_h(bb, thb[bb])
-            if jj == 0 and q + 1 < NQ:
-                mb(q + 1, nc.gpsimd)
-                exit_i(q + 1, 0)
-                exit_i(q + 1, 1)
-            if jj == 1 and q + 1 < NQ:
-                exit_z(q + 1, 0)
-                exit_z(q + 1, 1)
-            for qo in range(NQ):
-                if o_at[qo] == it:
-                    exit_o(qo, 0)
-                    exit_o(qo, 1)
-            if 8 <= it + 5 < NPAIR:
-                e1_pair(it + 5, "T", "act")
-            for bb in r2_at.get(it, []):
-                r2(bb)
+            qa = it if it < NQ else None
+            qk = it - 1 if 1 <= it <= NQ else None
+            bs = B_AT.get(it, [])
+            b0 = bs[0] if bs else None
+            todo = per_it[it]
+            if it + 2 < NQ:
+                load(mq, it + 2, mv, "m")
+            if it + 1 < NQ:
+                load(cq, it + 1, cv, "c")
+                load(nq, it + 1, nv, "n")
+
+            def act_jobs(k):
+                for z_ in range(k):
+                    tjob()
+
+            if it + 1 < NQ:
+                mb(it + 1, nc.gpsimd if MB_ON_GPSIMD else nc.vector)
+            first = min(4, todo) if it > 0 else 0
+            act_jobs(first)
+            todo -= first
+            if qa is not None:
+                v_a(2 * qa)
+                v_a(2 * qa + 1)
+            if CN_ON_GPSIMD and 2 <= it <= NQ + 1:
+                v_p(it - 2)
+            if qk is not None:
+                v_fn(qk)
+            if qa is not None:
+                v_mn(2 * qa)
+            if qk is not None:
+                v_nn(qk)
+            startup(it, 0)
+            if qk is not None:
+                v_fc(qk)
+            if qa is not None:
+                v_mn(2 * qa + 1)
+            startup(it, 1)
+            startup(it, 2)
+            if qk is not None:
+                v_iz(2 * qk)
+            if b0 is not None:
+                v_p2(b0)
+            if qk is not None:
+                v_iz(2 * qk + 1)
+            if b0 is not None:
+                v_h(2 * b0)
+            if qk is not None:
+                v_cn(qk)
+            if b0 is not None:
+                v_h(2 * b0 + 1)
+            if qk is not None and not CN_ON_GPSIMD:
+                v_p(qk)
+            startup(it, 3)
+            act_jobs(todo)
+            fresh = range(CHUNKS[ln_at[it]][0], CHUNKS[ln_at[it]][1]) if it in ln_at else []
+            for bq in B_AT.get(it + 1, []):
+                if bq not in fresh:
+                    s_r2(bq)
             if it in ln_at:
-                ln(ln_at[it])
-            if jj == 1 and 3 <= q + 2 < NQ:
-                quant(q + 2)
-            if jj == 0:
-                if q + 4 < NQ:
-                    load(xq, q + 4, xv, "x")
-                    load(hq, q + 4, hv, "h")
-                if q + 2 < NQ:
-                    load(mq, q + 2, mv, "m")
-            if jj == 1 and q + 2 < NQ:
-                load(cq, q + 2, cv, "c")
-                load(nq, q + 2, nv, "n")
+                s_ln(ln_at[it])
+            for bq in B_AT.get(it + 1, []):
+                if bq in fresh:
+                    s_r2(bq)
+            for bq in bs[1:]:
+                v_p2(bq)
+                v_h(2 * bq)
+                v_h(2 * bq + 1)
+            if 3 <= it + 2 < NQ:
+                quant(it + 2)

@@ -25,9 +25,13 @@ CHUNKS = [(0, 3), (3, 6), (6, 8)]
 B_AT = {5: [0], 6: [1], 7: [2], 8: [3, 4], 9: [5, 6, 7]}
 NITER = NQ + 2
 DUP = 0
-P2_ON_GPSIMD = False
+P2_ON_GPSIMD = True
 CN_ON_GPSIMD = False
 MB_ON_GPSIMD = True
+D_EXIT_ON_VECTOR = False
+SQ_ON_GPSIMD = True
+SQ_G_UPTO = 6
+P2_G_UPTO = 5
 GI, GF, GZ, GO, GN = 0, 2, 4, 6, 8
 NRING = 6
 
@@ -207,7 +211,10 @@ def tile_slstmcell_t_kernel(tc, x, h, c, n, m, W_i, b_i, W_f, b_f, W_o, b_o, W_z
 
             def drain():
                 dst[(q, blk % 2)] = gt.tile([P, 512], F32, name=tag, tag=tag + str(blk % 2), bufs=bufs)
-                nc.scalar.activation(out=dst[(q, blk % 2)][:], in_=tb_of[key][:], func=func, bias=bias, scale=scale)
+                if D_EXIT_ON_VECTOR and tag == "dT":
+                    nc.vector.tensor_scalar(out=dst[(q, blk % 2)][:], in0=tb_of[key][:], scalar1=bias, scalar2=None, op0=ALU.add)
+                else:
+                    nc.scalar.activation(out=dst[(q, blk % 2)][:], in_=tb_of[key][:], func=func, bias=bias, scale=scale)
 
             jobs.append((pe, drain))
 
@@ -328,7 +335,13 @@ def tile_slstmcell_t_kernel(tc, x, h, c, n, m, W_i, b_i, W_f, b_f, W_o, b_o, W_z
             nc.vector.scalar_tensor_tensor(out=nnq[q][:], in0=e1q[q][:], scalar=1.0, in1=fnq[q][:], op0=ALU.min, op1=ALU.add)
             store(2, q, nnq[q])
             sqq[q] = ring.tile([P, QW], F32, name="sq", tag="sq")
-            nc.scalar.activation(out=sqq[q][:], in_=nnq[q][:], func=ACT.Square, bias=epsc[:], scale=1.0)
+            if SQ_ON_GPSIMD and q < SQ_G_UPTO:
+                for t in range(4):
+                    cols = slice(t * DIM, (t + 1) * DIM)
+                    nc.gpsimd.tensor_scalar(out=sqq[q][:, cols], in0=nnq[q][:, cols], scalar1=EPS, scalar2=1.0, op0=ALU.add, op1=ALU.mult)
+                    nc.gpsimd.tensor_tensor(out=sqq[q][:, cols], in0=sqq[q][:, cols], in1=sqq[q][:, cols], op=ALU.mult)
+            else:
+                nc.scalar.activation(out=sqq[q][:], in_=nnq[q][:], func=ACT.Square, bias=epsc[:], scale=1.0)
 
         def v_fc(q):
             nc.vector.scalar_tensor_tensor(out=e2q[q][:], in0=e2q[q][:], scalar=1.0, in1=cq[q][:], op0=ALU.min, op1=ALU.mult)
@@ -351,7 +364,7 @@ def tile_slstmcell_t_kernel(tc, x, h, c, n, m, W_i, b_i, W_f, b_f, W_o, b_o, W_z
         r2done, p2done = {}, {}
 
         def g_p2(q):
-            if P2_ON_GPSIMD and q in pq and q in r2done and q not in p2done:
+            if P2_ON_GPSIMD and q < P2_G_UPTO and q in pq and q in r2done and q not in p2done:
                 p2done[q] = True
                 for t in range(4):
                     cols = slice(t * DIM, (t + 1) * DIM)
@@ -372,7 +385,7 @@ def tile_slstmcell_t_kernel(tc, x, h, c, n, m, W_i, b_i, W_f, b_f, W_o, b_o, W_z
             g_p2(q)
 
         def v_p2(q):
-            if not P2_ON_GPSIMD:
+            if not (P2_ON_GPSIMD and q < P2_G_UPTO):
                 nc.vector.tensor_tensor(out=sqq[q][:], in0=pq[q][:], in1=sqq[q][:], op=ALU.mult)
 
         def v_h(j):

@@ -25,11 +25,12 @@ CHUNKS = [(0, 3), (3, 6), (6, 8)]
 B_AT = {5: [0], 6: [1], 7: [2], 8: [3, 4], 9: [5, 6, 7]}
 NITER = NQ + 2
 DUP = 0
-P2_ON_GPSIMD = True
+P2_ON_GPSIMD = False
 CN_ON_GPSIMD = False
-MB_ON_GPSIMD = True
+MB_ON_GPSIMD = False
+FB_QUADS = []
 D_EXIT_ON_VECTOR = False
-SQ_ON_GPSIMD = True
+SQ_ON_GPSIMD = False
 SQ_G_UPTO = 6
 P2_G_UPTO = 5
 GI, GF, GZ, GO, GN = 0, 2, 4, 6, 8
@@ -80,7 +81,7 @@ def tile_slstmcell_t_kernel(tc, x, h, c, n, m, W_i, b_i, W_f, b_f, W_o, b_o, W_z
         gw = wst.tile([P, 10 * 512], BF16, name="gw", align_bytes=64)
 
         xq, hq, mq, cq, nq, mbq, gq = {}, {}, {}, {}, {}, {}, {}
-        dT, zT, thT = {}, {}, {}
+        dT, zT, thT, fT = {}, {}, {}, {}
         e1q, e2q, fnq, nnq, cnq, mnq, hhq, pq, sqq, a_t = {}, {}, {}, {}, {}, {}, {}, {}, {}, {}
         quantised = {}
 
@@ -224,6 +225,10 @@ def tile_slstmcell_t_kernel(tc, x, h, c, n, m, W_i, b_i, W_f, b_f, W_o, b_o, W_z
             for r in range(2):
                 add_exit(q, GI + r, dT, ACT.Identity, bd[:, r : r + 1], 1.0, "dT", 2, blk2=GN + r)
 
+        def add_exit_f(q):
+            for r in range(2):
+                add_exit(q, GF + r, fT, ACT.Identity, bcol[:, GF + r : GF + r + 1], 1.0, "fT", 2)
+
         def add_exit_z(q):
             for r in range(2):
                 add_exit(q, GZ + r, zT, ACT.Tanh, bcol[:, GZ + r : GZ + r + 1], 1.0, "zT", 2)
@@ -302,14 +307,20 @@ def tile_slstmcell_t_kernel(tc, x, h, c, n, m, W_i, b_i, W_f, b_f, W_o, b_o, W_z
             return t[:, (j % 2) * PW : (j % 2 + 1) * PW]
 
         def mb(q, eng):
+            if q in FB_QUADS:
+                return
             mbq[q] = wk.tile([P, QW], F32, name="mb", tag="mb")
-            for t in range(4):
-                cols = slice(t * DIM, (t + 1) * DIM)
-                eng.tensor_tensor(out=mbq[q][:, cols], in0=mq[q][:, cols], in1=bfb[:], op=ALU.add)
+            eng.tensor_tensor(
+                out=mbq[q][:].rearrange("p (t d) -> p t d", t=4),
+                in0=mq[q][:].rearrange("p (t d) -> p t d", t=4),
+                in1=bfb[:].unsqueeze(1).to_broadcast([P, 4, DIM]),
+                op=ALU.add,
+            )
 
         def v_a(j):
             a_t[j] = wk.tile([P, PW], F32, name="a", tag="a")
-            nc.vector.tensor_tensor(out=a_t[j][:], in0=bankof[("F", j)][:], in1=half(mbq[j // 2], j), op=ALU.add)
+            other = mq[j // 2] if j // 2 in FB_QUADS else mbq[j // 2]
+            nc.vector.tensor_tensor(out=a_t[j][:], in0=bankof[("F", j)][:], in1=half(other, j), op=ALU.add)
             used()
 
         def v_mn(j):
@@ -402,6 +413,8 @@ def tile_slstmcell_t_kernel(tc, x, h, c, n, m, W_i, b_i, W_f, b_f, W_o, b_o, W_z
         add_e1_pair(0, "act")
         add_e1_pair(1, "dve")
         add_exit_d(0)
+        if 0 in FB_QUADS:
+            add_exit_f(0)
         add_e1_pair(2, "dve")
         add_e1_pair(3, "dve")
         add_e1_w(2, "act")
@@ -412,6 +425,8 @@ def tile_slstmcell_t_kernel(tc, x, h, c, n, m, W_i, b_i, W_f, b_f, W_o, b_o, W_z
             n0 = len(jobs)
             if it + 1 < NQ:
                 add_exit_d(it + 1)
+                if it + 1 in FB_QUADS:
+                    add_exit_f(it + 1)
             if it < NQ:
                 add_exit_z(it)
             for bq in B_AT.get(it + 1, []):
@@ -424,8 +439,12 @@ def tile_slstmcell_t_kernel(tc, x, h, c, n, m, W_i, b_i, W_f, b_f, W_o, b_o, W_z
             per_it[it] = len(jobs) - n0
         for it in range(NITER):
             if it < NQ:
-                add_f(2 * it)
-                add_f(2 * it + 1)
+                if it in FB_QUADS:
+                    add_back("F", fT, 2 * it, False)
+                    add_back("F", fT, 2 * it + 1, False)
+                else:
+                    add_f(2 * it)
+                    add_f(2 * it + 1)
                 add_back("D", dT, 2 * it, True)
                 add_back("D", dT, 2 * it + 1, True)
             if 1 <= it <= NQ:
@@ -491,6 +510,9 @@ def tile_slstmcell_t_kernel(tc, x, h, c, n, m, W_i, b_i, W_f, b_f, W_o, b_o, W_z
         mb(0, nc.vector)
         tjob()
         tjob()
+        if 0 in FB_QUADS:
+            tjob()
+            tjob()
         pump()
 
         def startup(it, pos):

from contextlib import ExitStack

import concourse.mybir as mybir
from concourse.masks import make_identity

F32 = mybir.dt.float32
BF16 = mybir.dt.bfloat16
U32 = mybir.dt.uint32
U8 = mybir.dt.uint8
FP8X4 = mybir.dt.float8_e4m3fn_x4
ACT = mybir.ActivationFunctionType
ALU = mybir.AluOpType

P = 128
B = 4096
DIM = 256
NT = B // P
NQ = NT // 4
PW = 2 * DIM
QW = 4 * DIM
EPS = 1e-6
FLOPS = 2 * B * 2 * DIM * 4 * DIM

CHUNKS = [(0, 3), (3, 6), (6, 8)]
B_AT = {5: [0], 6: [1], 7: [2], 8: [3, 4], 9: [5, 6, 7]}
NITER = NQ + 2
DUP = 0
P2_ON_GPSIMD = False
CN_ON_GPSIMD = False
MB_ON_GPSIMD = False
FB_QUADS = []
D_EXIT_ON_VECTOR = False
SQ_ON_GPSIMD = False
SQ_G_UPTO = 6
P2_G_UPTO = 5
GI, GF, GZ, GO, GN = 0, 2, 4, 6, 8
NRING = 6


def tile_slstmcell_t_kernel(tc, x, h, c, n, m, W_i, b_i, W_f, b_f, W_o, b_o, W_z, b_z, out):
    nc = tc.nc
    ln_at = {}
    for ci, (s, e) in enumerate(CHUNKS):
        ln_at[e] = ci

    xv = x.rearrange("(p t) d -> p (t d)", t=NT)
    hv = h.rearrange("(p t) d -> p (t d)", t=NT)
    cv = c.rearrange("(p t) d -> p (t d)", t=NT)
    nv = n.rearrange("(p t) d -> p (t d)", t=NT)
    mv = m.rearrange("(p t) d -> p (t d)", t=NT)
    ov = out.rearrange("g (p t) d -> g p (t d)", t=NT)

    with ExitStack() as ctx:
        ctx.enter_context(tc.manual_schedule())
        const = ctx.enter_context(tc.tile_pool(name="const", bufs=1))
        ps = ctx.enter_context(tc.psum_pool(name="ps", bufs=1))
        ld = ctx.enter_context(tc.tile_pool(name="ld", bufs=3))
        grp = ctx.enter_context(tc.tile_pool(name="grp", bufs=2))
        wst = ctx.enter_context(tc.tile_pool(name="wst", bufs=1))
        gt = ctx.enter_context(tc.tile_pool(name="gt", bufs=2))
        wk = ctx.enter_context(tc.tile_pool(name="wk", bufs=2))
        ost = ctx.enter_context(tc.tile_pool(name="ost", bufs=2))
        ring = ctx.enter_context(tc.tile_pool(name="ring", bufs=6))

        ident32 = const.tile([P, P], F32, name="ident32")
        identb = const.tile([P, P], BF16, name="identb")
        negi = const.tile([P, P], BF16, name="negi")
        brow = const.tile([P, P], BF16, name="brow")
        bcol = const.tile([P, 8], F32, name="bcol")
        bhalf = const.tile([P, 2], F32, name="bhalf")
        bd = const.tile([P, 2], F32, name="bd")
        epsc = const.tile([P, 1], F32, name="epsc")
        bfb = const.tile([P, DIM], BF16, name="bfb")
        bfrow = const.tile([P, DIM], BF16, name="bfrow")
        ones = const.tile([P, P], BF16, name="ones")
        wc = const.tile([P, 10 * P], U32, name="wc", align_bytes=64)
        wscl = const.tile([P, 10 * P], U8, name="wscl", align_bytes=64)
        codes = const.tile([P, B], U32, name="codes", align_bytes=64)
        scl = const.tile([P, B], U8, name="scl", align_bytes=64)
        w_sb = wst.tile([P, 8 * 512], BF16, name="w_sb")
        gw = wst.tile([P, 10 * 512], BF16, name="gw", align_bytes=64)

        xq, hq, mq, cq, nq, mbq, gq = {}, {}, {}, {}, {}, {}, {}
        dT, zT, thT, fT = {}, {}, {}, {}
        e1q, e2q, fnq, nnq, cnq, mnq, hhq, pq, sqq, a_t = {}, {}, {}, {}, {}, {}, {}, {}, {}, {}
        quantised = {}

        fills = []
        state = {"filled": 0, "used": 0, "tpe": 0, "tact": 0}
        bankof = {}
        jobs = []

        def pump():
            while fills and state["filled"] - state["used"] < NRING:
                if not fills[0]():
                    break
                fills.pop(0)
                state["filled"] += 1

        def used():
            state["used"] += 1
            pump()

        def tpump():
            while state["tpe"] < len(jobs) and state["tpe"] - state["tact"] < 2:
                if not jobs[state["tpe"]][0]():
                    break
                state["tpe"] += 1

        def tjob():
            tpump()
            assert state["tpe"] > state["tact"], "job not ready"
            jobs[state["tact"]][1]()
            state["tact"] += 1
            tpump()
            pump()

        def load(dst, q, src, tag):
            dst[q] = ld.tile([P, QW], BF16, name=tag + "q", tag=tag)
            nc.sync.dma_start(out=dst[q][:], in_=src[:, q * QW : (q + 1) * QW])

        def store(g, q, t):
            nc.sync.dma_start(out=ov[g, :, q * QW : (q + 1) * QW], in_=t[:])

        tb_of = {}

        def add_e1(key, ins_fn, out_fn, eng, ready_fn):
            def pe():
                if not ready_fn():
                    return False
                tp = ps.tile([P, 512], F32, name="bank_T", tag="T", bufs=2)
                tb_of[key] = tp
                for i, src in enumerate(ins_fn()):
                    nc.tensor.transpose(tp[:, i * P : (i + 1) * P], src, ident32[:])
                return True

            def drain():
                src = tb_of[key][:].rearrange("p (s u c) -> p s c u", s=2, u=2)
                if eng == "act":
                    nc.scalar.copy(out=out_fn(), in_=src)
                else:
                    nc.vector.tensor_copy(out=out_fn(), in_=src)

            jobs.append((pe, drain))

        def add_e1_w(k, eng):
            w32 = w_sb[:].bitcast(F32)
            gw32 = gw[:, 0 : 8 * 512].bitcast(F32).rearrange("p (s c u) -> p s c u", s=8, u=2)
            add_e1(
                ("w", k),
                lambda: [w32[:, (2 * k + s) * 256 + u * P : (2 * k + s) * 256 + (u + 1) * P] for s in range(2) for u in range(2)],
                lambda: gw32[:, 2 * k : 2 * k + 2],
                eng,
                lambda: True,
            )

        def add_e1_pair(j, eng):
            q, jj = j // 2, j % 2

            def ins():
                x32 = xq[q][:].bitcast(F32)
                h32 = hq[q][:].bitcast(F32)
                res = []
                for tt in range(2):
                    t = 2 * jj + tt
                    res.append(x32[:, t * P : (t + 1) * P])
                    res.append(h32[:, t * P : (t + 1) * P])
                return res

            def dst():
                if jj == 0:
                    gq[q] = grp.tile([P, 4 * 512], BF16, name="g", tag="g", align_bytes=64)
                g32 = gq[q][:].bitcast(F32).rearrange("p (t c u) -> p t c u", t=4, u=2)
                return g32[:, 2 * jj : 2 * jj + 2]

            add_e1(("x", j), ins, dst, eng, lambda: q in xq and q in hq)
            if jj == 1 and q + 3 < NQ:
                pe_, drain_ = jobs.pop()

                def drain_and_load():
                    drain_()
                    load(xq, q + 3, xv, "x")
                    load(hq, q + 3, hv, "h")

                jobs.append((pe_, drain_and_load))

        def add_exit(q, blk, dst, func, bias, scale, tag, bufs, blk2=None):
            key = (tag, q, blk)

            def pe():
                if q not in quantised or blk not in quantised_w or (blk2 is not None and blk2 not in quantised_w):
                    return False
                tbk = ps.tile([P, 512], F32, name="bank_T", tag="T", bufs=2)
                tb_of[key] = tbk
                seq = [(blk, True, True)] * DUP
                if blk2 is None:
                    seq.append((blk, True, True))
                else:
                    seq.append((blk, True, False))
                    seq.append((blk2, False, True))
                for bl, st, sp in seq:
                    nc.tensor.matmul_mx(
                        out=tbk[:],
                        lhsT=wc[:, bl * P : (bl + 1) * P].bitcast(FP8X4),
                        lhsT_scale=wscl[:, bl * P : (bl + 1) * P],
                        rhs=codes[:, q * 512 : (q + 1) * 512].bitcast(FP8X4),
                        rhs_scale=scl[:, q * 512 : (q + 1) * 512],
                        start=st,
                        stop=sp,
                    )
                return True

            def drain():
                dst[(q, blk % 2)] = gt.tile([P, 512], F32, name=tag, tag=tag + str(blk % 2), bufs=bufs)
                if D_EXIT_ON_VECTOR and tag == "dT":
                    nc.vector.tensor_scalar(out=dst[(q, blk % 2)][:], in0=tb_of[key][:], scalar1=bias, scalar2=None, op0=ALU.add)
                else:
                    nc.scalar.activation(out=dst[(q, blk % 2)][:], in_=tb_of[key][:], func=func, bias=bias, scale=scale)

            jobs.append((pe, drain))

        quantised_w = {}

        def add_exit_d(q):
            for r in range(2):
                add_exit(q, GI + r, dT, ACT.Identity, bd[:, r : r + 1], 1.0, "dT", 2, blk2=GN + r)

        def add_exit_f(q):
            for r in range(2):
                add_exit(q, GF + r, fT, ACT.Identity, bcol[:, GF + r : GF + r + 1], 1.0, "fT", 2)

        def add_exit_z(q):
            for r in range(2):
                add_exit(q, GZ + r, zT, ACT.Tanh, bcol[:, GZ + r : GZ + r + 1], 1.0, "zT", 2)

        def add_exit_o(q):
            for r in range(2):
                add_exit(q, GO + r, thT, ACT.Tanh, bhalf[:, r : r + 1], 0.5, "thT", 3)

        def quant(q):
            nc.vector.quantize_mx(
                out=codes[:, q * 512 : (q + 1) * 512].bitcast(FP8X4),
                scales=scl[:, q * 512 : (q + 1) * 512],
                in_=gq[q][:],
            )
            quantised[q] = True
            tpump()
            pump()

        def quant_w(s0, nblk):
            nc.vector.quantize_mx(
                out=wc[:, s0 * P : (s0 + nblk) * P].bitcast(FP8X4),
                scales=wscl[:, s0 * P : (s0 + nblk) * P],
                in_=gw[:, s0 * 512 : (s0 + nblk) * 512],
            )
            for bl in range(s0, s0 + nblk):
                quantised_w[bl] = True
            tpump()
            pump()

        def new_bank(key):
            bankof[key] = ps.tile([P, 512], F32, name="bank_B", tag="B", bufs=NRING)
            return bankof[key]

        def add_f(j):
            def go():
                if j // 2 not in quantised or GF not in quantised_w:
                    return False
                bk = new_bank(("F", j))
                for tt in range(2):
                    t = 2 * j + tt
                    nc.tensor.matmul_mx(
                        out=bk[:, tt * DIM : (tt + 1) * DIM],
                        lhsT=codes[:, t * P : (t + 1) * P].bitcast(FP8X4),
                        lhsT_scale=scl[:, t * P : (t + 1) * P],
                        rhs=wc[:, GF * P : (GF + 2) * P].bitcast(FP8X4),
                        rhs_scale=wscl[:, GF * P : (GF + 2) * P],
                        start=True,
                        stop=True,
                    )
                return True

            fills.append(go)

        def add_back(kind, src, j, minus_m):
            q, jj = j // 2, j % 2

            def go():
                if (q, 0) not in src or (q, 1) not in src:
                    return False
                bk = new_bank((kind, j))
                if minus_m:
                    nc.tensor.matmul(out=bk[:], lhsT=negi[:], rhs=mq[q][:, jj * PW : (jj + 1) * PW], start=True, stop=False)
                for tt in range(2):
                    for r in range(2):
                        o = bk[:, tt * DIM + r * P : tt * DIM + (r + 1) * P]
                        i = src[(q, r)][:, (2 * jj + tt) * P : (2 * jj + tt + 1) * P]
                        if minus_m:
                            nc.tensor.matmul(out=o, lhsT=i, rhs=ident32[:], is_transpose=True, start=False, stop=(tt == 1 and r == 1))
                        else:
                            nc.tensor.transpose(o, i, ident32[:])
                return True

            fills.append(go)

        def half(t, j):
            return t[:, (j % 2) * PW : (j % 2 + 1) * PW]

        def mb(q, eng):
            if q in FB_QUADS:
                return
            mbq[q] = wk.tile([P, QW], F32, name="mb", tag="mb")
            eng.tensor_tensor(
                out=mbq[q][:].rearrange("p (t d) -> p t d", t=4),
                in0=mq[q][:].rearrange("p (t d) -> p t d", t=4),
                in1=bfb[:].unsqueeze(1).to_broadcast([P, 4, DIM]),
                op=ALU.add,
            )

        def v_a(j):
            a_t[j] = wk.tile([P, PW], F32, name="a", tag="a")
            other = mq[j // 2] if j // 2 in FB_QUADS else mbq[j // 2]
            nc.vector.tensor_tensor(out=a_t[j][:], in0=bankof[("F", j)][:], in1=half(other, j), op=ALU.add)
            used()

        def v_mn(j):
            q = j // 2
            if j % 2 == 0:
                mnq[q] = ost.tile([P, QW], F32, name="mn", tag="mn")
                e1q[q] = wk.tile([P, QW], F32, name="e1", tag="e1")
                e2q[q] = wk.tile([P, QW], F32, name="e2", tag="e2")
            d = bankof[("D", j)]
            nc.vector.scalar_tensor_tensor(out=half(mnq[q], j), in0=d[:], scalar=0.0, in1=a_t[j][:], op0=ALU.max, op1=ALU.add)
            nc.scalar.activation(out=half(e1q[q], j), in_=d[:], func=ACT.Exp, scale=1.0)
            nc.scalar.activation(out=half(e2q[q], j), in_=d[:], func=ACT.Exp, scale=-1.0)
            used()
            if j % 2 == 1:
                store(3, q, mnq[q])

        def v_fn(q):
            fnq[q] = wk.tile([P, QW], F32, name="fn", tag="fn")
            nc.vector.scalar_tensor_tensor(out=fnq[q][:], in0=e2q[q][:], scalar=1.0, in1=nq[q][:], op0=ALU.min, op1=ALU.mult)

        def v_nn(q):
            nnq[q] = ost.tile([P, QW], F32, name="nn", tag="nn", bufs=3 if CN_ON_GPSIMD else 2)
            nc.vector.scalar_tensor_tensor(out=nnq[q][:], in0=e1q[q][:], scalar=1.0, in1=fnq[q][:], op0=ALU.min, op1=ALU.add)
            store(2, q, nnq[q])
            sqq[q] = ring.tile([P, QW], F32, name="sq", tag="sq")
            if SQ_ON_GPSIMD and q < SQ_G_UPTO:
                for t in range(4):
                    cols = slice(t * DIM, (t + 1) * DIM)
                    nc.gpsimd.tensor_scalar(out=sqq[q][:, cols], in0=nnq[q][:, cols], scalar1=EPS, scalar2=1.0, op0=ALU.add, op1=ALU.mult)
                    nc.gpsimd.tensor_tensor(out=sqq[q][:, cols], in0=sqq[q][:, cols], in1=sqq[q][:, cols], op=ALU.mult)
            else:
                nc.scalar.activation(out=sqq[q][:], in_=nnq[q][:], func=ACT.Square, bias=epsc[:], scale=1.0)

        def v_fc(q):
            nc.vector.scalar_tensor_tensor(out=e2q[q][:], in0=e2q[q][:], scalar=1.0, in1=cq[q][:], op0=ALU.min, op1=ALU.mult)

        def v_iz(j):
            e1h = half(e1q[j // 2], j)
            nc.vector.scalar_tensor_tensor(out=e1h, in0=e1h, scalar=1.0, in1=bankof[("Z", j)][:], op0=ALU.min, op1=ALU.mult)
            used()

        def v_cn(q):
            cnq[q] = ost.tile([P, QW], F32, name="cn", tag="cn", bufs=3 if CN_ON_GPSIMD else 2)
            if CN_ON_GPSIMD:
                for t in range(4):
                    cols = slice(t * DIM, (t + 1) * DIM)
                    nc.gpsimd.tensor_tensor(out=cnq[q][:, cols], in0=e1q[q][:, cols], in1=e2q[q][:, cols], op=ALU.add)
            else:
                nc.vector.tensor_tensor(out=cnq[q][:], in0=e1q[q][:], in1=e2q[q][:], op=ALU.add)
            store(1, q, cnq[q])

        r2done, p2done = {}, {}

        def g_p2(q):
            if P2_ON_GPSIMD and q < P2_G_UPTO and q in pq and q in r2done and q not in p2done:
                p2done[q] = True
                for t in range(4):
                    cols = slice(t * DIM, (t + 1) * DIM)
                    nc.gpsimd.tensor_tensor(out=sqq[q][:, cols], in0=pq[q][:, cols], in1=sqq[q][:, cols], op=ALU.mult)

        def v_p(q):
            pq[q] = ring.tile([P, QW], F32, name="p", tag="p")
            nc.vector.scalar_tensor_tensor(out=pq[q][:], in0=nnq[q][:], scalar=EPS, in1=cnq[q][:], op0=ALU.add, op1=ALU.mult)
            g_p2(q)

        def s_ln(ci):
            for q in range(CHUNKS[ci][0], CHUNKS[ci][1]):
                nc.scalar.activation(out=sqq[q][:], in_=sqq[q][:], func=ACT.Ln, scale=2.0)

        def s_r2(q):
            nc.scalar.activation(out=sqq[q][:], in_=sqq[q][:], func=ACT.Exp, scale=-1.0)
            r2done[q] = True
            g_p2(q)

        def v_p2(q):
            if not (P2_ON_GPSIMD and q < P2_G_UPTO):
                nc.vector.tensor_tensor(out=sqq[q][:], in0=pq[q][:], in1=sqq[q][:], op=ALU.mult)

        def v_h(j):
            q = j // 2
            if j % 2 == 0:
                hhq[q] = ost.tile([P, QW], F32, name="hh", tag="hh")
            nc.vector.scalar_tensor_tensor(out=half(hhq[q], j), in0=bankof[("TH", j)][:], scalar=1.0, in1=half(sqq[q], j), op0=ALU.add, op1=ALU.mult)
            used()
            if j % 2 == 1:
                store(0, q, hhq[q])

        add_e1_w(0, "act")
        add_e1_w(1, "dve")
        add_e1_pair(0, "act")
        add_e1_pair(1, "dve")
        add_exit_d(0)
        if 0 in FB_QUADS:
            add_exit_f(0)
        add_e1_pair(2, "dve")
        add_e1_pair(3, "dve")
        add_e1_w(2, "act")
        add_e1_pair(4, "dve")
        add_e1_pair(5, "dve")
        per_it = {}
        for it in range(NITER):
            n0 = len(jobs)
            if it + 1 < NQ:
                add_exit_d(it + 1)
                if it + 1 in FB_QUADS:
                    add_exit_f(it + 1)
            if it < NQ:
                add_exit_z(it)
            for bq in B_AT.get(it + 1, []):
                add_exit_o(bq)
            if it + 3 < NQ:
                add_e1_pair(2 * (it + 3), "act")
                add_e1_pair(2 * (it + 3) + 1, "act")
            if it == 0:
                add_e1_w(3, "act")
            per_it[it] = len(jobs) - n0
        for it in range(NITER):
            if it < NQ:
                if it in FB_QUADS:
                    add_back("F", fT, 2 * it, False)
                    add_back("F", fT, 2 * it + 1, False)
                else:
                    add_f(2 * it)
                    add_f(2 * it + 1)
                add_back("D", dT, 2 * it, True)
                add_back("D", dT, 2 * it + 1, True)
            if 1 <= it <= NQ:
                add_back("Z", zT, 2 * (it - 1), False)
                add_back("Z", zT, 2 * (it - 1) + 1, False)
            for bq in B_AT.get(it, []):
                add_back("TH", thT, 2 * bq, False)
                add_back("TH", thT, 2 * bq + 1, False)

        make_identity(nc, ident32[:])
        nc.vector.memset(brow[:], 0.0)
        nc.vector.memset(epsc[:], EPS)
        nc.vector.memset(bfrow[:], 0.0)
        nc.vector.memset(ones[:], 1.0)
        nc.scalar.dma_start(out=brow[0:2, :], in_=b_i.rearrange("(r c) -> r c", r=2))
        nc.scalar.dma_start(out=brow[2:4, :], in_=b_f.rearrange("(r c) -> r c", r=2))
        nc.scalar.dma_start(out=bfrow[0:1, :], in_=b_f.rearrange("(r c) -> r c", r=1))
        nc.scalar.dma_start(out=brow[4:6, :], in_=b_z.rearrange("(r c) -> r c", r=2))
        nc.scalar.dma_start(out=brow[6:8, :], in_=b_o.rearrange("(r c) -> r c", r=2))

        def load_w(s0, wg):
            nc.sync.dma_start(
                out=w_sb[:, s0 * 512 : (s0 + 2) * 512].rearrange("p (r k) -> p r k", r=2),
                in_=wg.rearrange("(r p) k -> p r k", p=P),
            )

        load_w(GI, W_i)
        load_w(GF, W_f)
        load(xq, 0, xv, "x")
        load(hq, 0, hv, "h")
        load(mq, 0, mv, "m")
        load(xq, 1, xv, "x")
        load(hq, 1, hv, "h")
        load_w(GZ, W_z)
        load(xq, 2, xv, "x")
        load(hq, 2, hv, "h")
        load(cq, 0, cv, "c")
        load(nq, 0, nv, "n")
        load(mq, 1, mv, "m")
        load_w(GO, W_o)

        nc.vector.tensor_copy(out=identb[:], in_=ident32[:])
        nc.vector.tensor_scalar(out=negi[:], in0=ident32[:], scalar1=-1.0, scalar2=None, op0=ALU.mult)
        tjob()
        tjob()
        nc.vector.tensor_scalar(out=gw[:, GN * 512 : (GN + 2) * 512], in0=gw[:, GF * 512 : (GF + 2) * 512], scalar1=-1.0, scalar2=None, op0=ALU.mult)
        quant_w(GI, 4)
        tjob()
        tjob()
        tb = ps.tile([P, 512], F32, name="bank_B", tag="B", bufs=NRING)
        tbb = tb[:].bitcast(BF16)
        nc.tensor.transpose(tbb[:, 0:P], brow[:], identb[:])
        nc.vector.tensor_copy(out=bcol[:], in_=tbb[:, 0:8])
        nc.tensor.matmul(out=tb[:, DIM : 2 * DIM], lhsT=ones[:], rhs=bfrow[:], start=True, stop=True)
        nc.vector.tensor_copy(out=bfb[:], in_=tb[:, DIM : 2 * DIM])
        nc.vector.tensor_scalar(out=bhalf[:], in0=bcol[:, GO : GO + 2], scalar1=0.5, scalar2=None, op0=ALU.mult)
        nc.vector.tensor_tensor(out=bd[:], in0=bcol[:, GI : GI + 2], in1=bcol[:, GF : GF + 2], op=ALU.subtract)
        state["filled"] += 1
        state["used"] += 1

        quant_w(GN, 2)
        quant(0)
        mb(0, nc.vector)
        tjob()
        tjob()
        if 0 in FB_QUADS:
            tjob()
            tjob()
        pump()

        def startup(it, pos):
            if it == 0 and pos == 0:
                tjob()
                tjob()
                tjob()
                tjob()
                tjob()
            if it == 0 and pos == 1:
                quant(1)
                quant_w(GZ, 2)
                quant(2)
            if it == 1 and pos == 3:
                quant_w(GO, 2)

        for it in range(NITER):
            qa = it if it < NQ else None
            qk = it - 1 if 1 <= it <= NQ else None
            bs = B_AT.get(it, [])
            b0 = bs[0] if bs else None
            todo = per_it[it]
            if it + 2 < NQ:
                load(mq, it + 2, mv, "m")
            if it + 1 < NQ:
                load(cq, it + 1, cv, "c")
                load(nq, it + 1, nv, "n")

            def act_jobs(k):
                for z_ in range(k):
                    tjob()

            if it + 1 < NQ:
                mb(it + 1, nc.gpsimd if MB_ON_GPSIMD else nc.vector)
            first = min(4, todo) if it > 0 else 0
            act_jobs(first)
            todo -= first
            if qa is not None:
                v_a(2 * qa)
                v_a(2 * qa + 1)
            if CN_ON_GPSIMD and 2 <= it <= NQ + 1:
                v_p(it - 2)
            if qk is not None:
                v_fn(qk)
            if qa is not None:
                v_mn(2 * qa)
            if qk is not None:
                v_nn(qk)
            startup(it, 0)
            if qk is not None:
                v_fc(qk)
            if qa is not None:
                v_mn(2 * qa + 1)
            startup(it, 1)
            startup(it, 2)
            if qk is not None:
                v_iz(2 * qk)
            if b0 is not None:
                v_p2(b0)
            if qk is not None:
                v_iz(2 * qk + 1)
            if b0 is not None:
                v_h(2 * b0)
            if qk is not None:
                v_cn(qk)
            if b0 is not None:
                v_h(2 * b0 + 1)
            if qk is not None and not CN_ON_GPSIMD:
                v_p(qk)
            startup(it, 3)
            act_jobs(todo)
            fresh = range(CHUNKS[ln_at[it]][0], CHUNKS[ln_at[it]][1]) if it in ln_at else []
            for bq in B_AT.get(it + 1, []):
                if bq not in fresh:
                    s_r2(bq)
            if it in ln_at:
                s_ln(ln_at[it])
            for bq in B_AT.get(it + 1, []):
                if bq in fresh:
                    s_r2(bq)
            for bq in bs[1:]:
                v_p2(bq)
                v_h(2 * bq)
                v_h(2 * bq + 1)
            if 3 <= it + 2 < NQ:
                quant(it + 2)
